import numpy as np
import ml_dtypes


def mxq(x, axis, fmt="e4m3"):
    dtype, down = {"e4m3": (ml_dtypes.float8_e4m3fn, 7), "e5m2": (ml_dtypes.float8_e5m2, 14)}[fmt]
    v = np.moveaxis(np.asarray(x, np.float32).astype(ml_dtypes.bfloat16).astype(np.float64), axis, -1)
    blocks = v.reshape(v.shape[:-1] + (-1, 32))
    amax = np.abs(blocks).max(-1, keepdims=True)
    byte = np.maximum(np.where(amax > 0, np.frexp(amax)[1] - 1 + 127, 0) - down, 1)
    scale = np.exp2(byte - 127.0)
    codes = (blocks / scale).astype(np.float32).astype(dtype).astype(np.float64)
    return np.moveaxis((codes * scale).reshape(v.shape), -1, axis)


WIDE = False


def mx_kscale(k):
    if not WIDE:
        return np.ones(k)
    levels = np.array([10, -10, 5, -5, 0])
    a = np.random.permutation(np.resize(levels, k // 512 * 4)).reshape(k // 512, 4)
    idx = np.arange(k)
    return np.exp2(a[idx // 512, idx % 128 // 32])


BF16 = ml_dtypes.bfloat16


def bf(x):
    return np.asarray(x, np.float32).astype(BF16)


def f64(x):
    return np.asarray(x).astype(np.float64)


LQ, LK, D, H, DK, DV = 8192, 1024, 128, 8, 128, 128
HV = H * DV
LN_EPS = 1e-5


def setup_inputs():
    s = mx_kscale(HV)
    return {"attn_out": bf(np.random.standard_normal((H, LQ, DV)) * 0.7 * s.reshape(H, DV)[:, None, :]),
            "residual": bf(np.random.standard_normal((LQ, D))),
            "proj_w": bf(np.random.standard_normal((HV, D)) / np.sqrt(HV) / s[:, None]),
            "proj_b": bf(np.random.standard_normal(D) * 0.3),
            "ln_g": bf(1.0 + 0.1 * np.random.standard_normal(D)),
            "ln_b": bf(0.1 * np.random.standard_normal(D))}


def reference(attn_out, residual, proj_w, proj_b, ln_g, ln_b):
    x = f64(attn_out).transpose(1, 0, 2).reshape(LQ, HV)
    y = (mxq(x, 1, "e4m3") @ mxq(f64(proj_w), 0, "e4m3")) + f64(proj_b) + f64(residual)
    mu = y.mean(-1, keepdims=True)
    var = ((y - mu) ** 2).mean(-1, keepdims=True)
    return (y - mu) / np.sqrt(var + LN_EPS) * f64(ln_g) + f64(ln_b)

@@ -1,0 +1,216 @@
+from contextlib import ExitStack
+
+import concourse.mybir as mybir
+from concourse.masks import make_identity
+
+FLOPS = 2 * 8192 * 1024 * 128
+
+F32 = mybir.dt.float32
+BF16 = mybir.dt.bfloat16
+U32 = mybir.dt.uint32
+U8 = mybir.dt.uint8
+FP8X4 = mybir.dt.float8_e4m3fn_x4
+ALU = mybir.AluOpType
+ACT = mybir.ActivationFunctionType
+
+P = 128
+HEADS = 8
+DV = 128
+D = 128
+TOKENS = 8192
+LN_EPS = 1e-5
+
+T_ALL = TOKENS // P
+WORDS = DV // 2
+HEAD_PAIRS = HEADS // 2
+PACK = 4
+PAIR_T = 2
+STEP_T = 4
+PAIRS = STEP_T // PAIR_T
+MAX_CHUNK_T = 16
+
+
+def chunk_sizes():
+    sizes = [STEP_T]
+    while sum(sizes) < T_ALL:
+        sizes.append(min(sum(sizes), MAX_CHUNK_T))
+    return sizes
+
+
+def tile_multiheadattention_pb_t_kernel(
+    tc, attn_out, residual, proj_w, proj_b, ln_g, ln_b, out
+):
+    nc = tc.nc
+    x_dram = attn_out.rearrange("h (p t) j -> p h t j", t=T_ALL)
+    res_dram = residual.rearrange("(p t) f -> p t f", t=T_ALL)
+    out_dram = out.rearrange("(p t) f -> p t f", t=T_ALL)
+
+    with ExitStack() as ctx:
+        consts = ctx.enter_context(tc.tile_pool(name="consts", bufs=1))
+        loads = ctx.enter_context(tc.tile_pool(name="loads", bufs=1))
+        quant = ctx.enter_context(tc.tile_pool(name="quant", bufs=3))
+        work = ctx.enter_context(tc.tile_pool(name="work", bufs=3))
+        stats = ctx.enter_context(tc.tile_pool(name="stats", bufs=4))
+        psum_t = ctx.enter_context(tc.psum_pool(name="psum_t", bufs=6))
+        psum_y = ctx.enter_context(tc.psum_pool(name="psum_y", bufs=2))
+
+        x_words = []
+        res_rows = []
+        t0 = 0
+        for c, chunk_t in enumerate(chunk_sizes()):
+            x_sb = loads.tile([P, HEADS * chunk_t * DV], BF16, name="x%d" % c)
+            nc.sync.dma_start(
+                out=x_sb[:].rearrange("p (h t j) -> p h t j", h=HEADS, t=chunk_t),
+                in_=x_dram[:, :, t0 : t0 + chunk_t, :],
+            )
+            res_sb = loads.tile([P, chunk_t, D], BF16, name="res%d" % c)
+            nc.sync.dma_start(out=res_sb[:], in_=res_dram[:, t0 : t0 + chunk_t, :])
+            chunk_words = x_sb[:].bitcast(F32).rearrange("p (h w) -> p h w", h=HEADS)
+            for s in range(chunk_t // STEP_T):
+                x_words.append(chunk_words[:, :, s * STEP_T * WORDS : (s + 1) * STEP_T * WORDS])
+                res_rows.append(res_sb[:, s * STEP_T : (s + 1) * STEP_T, :])
+            t0 += chunk_t
+
+        w_rows = consts.tile([P, HEAD_PAIRS, PACK, D], BF16)
+        for s in range(PAIR_T):
+            nc.scalar.dma_start(
+                out=w_rows[s * WORDS : (s + 1) * WORDS].rearrange(
+                    "p a (i e) f -> p (a i) (e f)", i=2
+                ),
+                in_=proj_w.rearrange("(h w e) f -> w h (e f)", h=HEADS, e=2),
+            )
+        bias_bc = consts.tile([P, D], BF16)
+        gain_bc = consts.tile([P, D], BF16)
+        shift_bc = consts.tile([P, D], BF16)
+        nc.scalar.dma_start(out=bias_bc[:], in_=proj_b.partition_broadcast(P))
+        nc.scalar.dma_start(out=gain_bc[:], in_=ln_g.partition_broadcast(P))
+        nc.scalar.dma_start(out=shift_bc[:], in_=ln_b.partition_broadcast(P))
+
+        ident = consts.tile([P, P], F32)
+        make_identity(nc, ident[:])
+        eps = consts.tile([P, 1], F32)
+        nc.vector.memset(eps[:], LN_EPS)
+
+        w_grouped = consts.tile([P, HEAD_PAIRS, PAIR_T, D, PACK], BF16, align_bytes=64)
+        nc.vector.memset(w_grouped[:], 0.0)
+        lower, upper = slice(0, WORDS), slice(WORDS, P)
+        nc.vector.tensor_copy(
+            out=w_grouped[lower, :, 0, :, :], in_=w_rows[lower].rearrange("p a v f -> p a f v")
+        )
+        nc.scalar.copy(
+            out=w_grouped[upper, :, 1, :, :], in_=w_rows[upper].rearrange("p a v f -> p a f v")
+        )
+        w_codes = consts.tile([P, HEAD_PAIRS, PAIR_T * D], U32, align_bytes=64)
+        w_scales = consts.tile([P, HEAD_PAIRS, PAIR_T * D], U8, align_bytes=64)
+        nc.vector.quantize_mx(
+            out=w_codes[:].rearrange("p a n -> p (a n)").bitcast(FP8X4),
+            scales=w_scales[:].rearrange("p a n -> p (a n)"),
+            in_=w_grouped[:].rearrange("p a s f v -> p (a s f v)"),
+        )
+
+        for step in range(T_ALL // STEP_T):
+            grouped = quant.tile([P, PAIRS * HEAD_PAIRS * P * PACK], BF16, align_bytes=64)
+            grouped_words = grouped[:].bitcast(F32).rearrange(
+                "p (q a c i) -> p q a c i", q=PAIRS, a=HEAD_PAIRS, i=2
+            )
+            x_codes = quant.tile([P, PAIRS, HEAD_PAIRS, P], U32, align_bytes=64)
+            x_scales = quant.tile([P, PAIRS, HEAD_PAIRS, P], U8, align_bytes=64)
+            for q in range(PAIRS):
+                pair_words = slice(q * PAIR_T * WORDS, (q + 1) * PAIR_T * WORDS)
+                for a0 in range(0, HEAD_PAIRS, 2):
+                    xt = psum_t.tile([P, 2, 2, P], F32)
+                    for u in range(2):
+                        for i in range(2):
+                            nc.tensor.transpose(
+                                xt[:, u, i, :],
+                                x_words[step][:, 2 * (a0 + u) + i, pair_words],
+                                ident[:],
+                            )
+                    nc.scalar.copy(
+                        out=grouped_words[:, q, a0 : a0 + 2, :, :],
+                        in_=xt[:].rearrange("p u i c -> p u c i"),
+                    )
+                width = HEAD_PAIRS * P * PACK
+                nc.vector.quantize_mx(
+                    out=x_codes[:, q].rearrange("p a c -> p (a c)").bitcast(FP8X4),
+                    scales=x_scales[:, q].rearrange("p a c -> p (a c)"),
+                    in_=grouped[:, q * width : (q + 1) * width],
+                )
+
+            y_ps = psum_y.tile([P, STEP_T, D], F32)
+            for q in range(PAIRS):
+                for a in range(HEAD_PAIRS):
+                    nc.tensor.matmul_mx(
+                        out=y_ps[:, q * PAIR_T : (q + 1) * PAIR_T, :].rearrange("p t f -> p (t f)"),
+                        lhsT=x_codes[:, q, a, :].bitcast(FP8X4),
+                        lhsT_scale=x_scales[:, q, a, :],
+                        rhs=w_codes[:, a, :].bitcast(FP8X4),
+                        rhs_scale=w_scales[:, a, :],
+                        start=(a == 0),
+                        stop=(a == HEAD_PAIRS - 1),
+                    )
+
+            res_bias = work.tile([P, STEP_T, D], F32)
+            nc.vector.tensor_tensor(
+                out=res_bias[:],
+                in0=res_rows[step],
+                in1=bias_bc[:].unsqueeze(1).to_broadcast([P, STEP_T, D]),
+                op=ALU.add,
+            )
+
+            y = work.tile([P, STEP_T, D], F32)
+            y_sum = stats.tile([P, STEP_T], F32)
+            for t in range(STEP_T):
+                nc.vector.scalar_tensor_tensor(
+                    out=y[:, t, :],
+                    in0=y_ps[:, t, :],
+                    scalar=1.0,
+                    in1=res_bias[:, t, :],
+                    op0=ALU.mult,
+                    op1=ALU.add,
+                    accum_out=y_sum[:, t : t + 1],
+                )
+            mean = stats.tile([P, STEP_T], F32)
+            nc.vector.tensor_scalar_mul(out=mean[:], in0=y_sum[:], scalar1=1.0 / D)
+
+            squares = work.tile([P, STEP_T, D], BF16)
+            sq_sum = stats.tile([P, STEP_T], F32)
+            for t in range(STEP_T):
+                nc.scalar.activation(
+                    out=squares[:, t, :],
+                    in_=y[:, t, :],
+                    func=ACT.Square,
+                    bias=mean[:, t : t + 1],
+                    scale=-1.0,
+                    accum_out=sq_sum[:, t : t + 1],
+                )
+            std = stats.tile([P, STEP_T], F32)
+            nc.scalar.activation(
+                out=std[:], in_=sq_sum[:], func=ACT.Sqrt, bias=eps[:], scale=1.0 / D
+            )
+            rstd = stats.tile([P, STEP_T], F32)
+            nc.vector.reciprocal(out=rstd[:], in_=std[:])
+
+            centred = work.tile([P, STEP_T, D], F32)
+            result = work.tile([P, STEP_T, D], F32)
+            for t in range(STEP_T):
+                nc.vector.scalar_tensor_tensor(
+                    out=centred[:, t, :],
+                    in0=y[:, t, :],
+                    scalar=mean[:, t : t + 1],
+                    in1=gain_bc[:],
+                    op0=ALU.subtract,
+                    op1=ALU.mult,
+                )
+            for t in range(STEP_T):
+                nc.vector.scalar_tensor_tensor(
+                    out=result[:, t, :],
+                    in0=centred[:, t, :],
+                    scalar=rstd[:, t : t + 1],
+                    in1=shift_bc[:],
+                    op0=ALU.mult,
+                    op1=ALU.add,
+                )
+            nc.sync.dma_start(
+                out=out_dram[:, step * STEP_T : (step + 1) * STEP_T, :], in_=result[:]
+            )

@@ -27,6 +27,8 @@ PACK = 4
 PAIR_T = 2
 STEP_T = 4
 PAIRS = STEP_T // PAIR_T
+STEPS = T_ALL // STEP_T
+BANK_HEAD_PAIRS = 2
 MAX_CHUNK_T = 16
 
 
@@ -48,11 +50,13 @@ def tile_multiheadattention_pb_t_kernel(
     with ExitStack() as ctx:
         consts = ctx.enter_context(tc.tile_pool(name="consts", bufs=1))
         loads = ctx.enter_context(tc.tile_pool(name="loads", bufs=1))
-        quant = ctx.enter_context(tc.tile_pool(name="quant", bufs=3))
-        work = ctx.enter_context(tc.tile_pool(name="work", bufs=3))
-        stats = ctx.enter_context(tc.tile_pool(name="stats", bufs=4))
+        quant = ctx.enter_context(tc.tile_pool(name="quant", bufs=2))
+        work = ctx.enter_context(tc.tile_pool(name="work", bufs=2))
+        stats = ctx.enter_context(tc.tile_pool(name="stats", bufs=3))
+        results = ctx.enter_context(tc.tile_pool(name="results", bufs=12))
         psum_t = ctx.enter_context(tc.psum_pool(name="psum_t", bufs=6))
         psum_y = ctx.enter_context(tc.psum_pool(name="psum_y", bufs=2))
+        ctx.enter_context(tc.manual_schedule())
 
         x_words = []
         res_rows = []
@@ -108,109 +112,153 @@ def tile_multiheadattention_pb_t_kernel(
             in_=w_grouped[:].rearrange("p a s f v -> p (a s f v)"),
         )
 
-        for step in range(T_ALL // STEP_T):
-            grouped = quant.tile([P, PAIRS * HEAD_PAIRS * P * PACK], BF16, align_bytes=64)
-            grouped_words = grouped[:].bitcast(F32).rearrange(
-                "p (q a c i) -> p q a c i", q=PAIRS, a=HEAD_PAIRS, i=2
-            )
-            x_codes = quant.tile([P, PAIRS, HEAD_PAIRS, P], U32, align_bytes=64)
-            x_scales = quant.tile([P, PAIRS, HEAD_PAIRS, P], U8, align_bytes=64)
+        xt_banks, grouped, x_codes, x_scales, y_ps = {}, {}, {}, {}, {}
+        res_bias, y, y_sum, mean, rstd, centred = {}, {}, {}, {}, {}, {}
+
+        def transposes(step):
             for q in range(PAIRS):
                 pair_words = slice(q * PAIR_T * WORDS, (q + 1) * PAIR_T * WORDS)
-                for a0 in range(0, HEAD_PAIRS, 2):
-                    xt = psum_t.tile([P, 2, 2, P], F32)
-                    for u in range(2):
+                for b in range(HEAD_PAIRS // BANK_HEAD_PAIRS):
+                    xt = psum_t.tile([P, BANK_HEAD_PAIRS, 2, P], F32, name="xt")
+                    for u in range(BANK_HEAD_PAIRS):
                         for i in range(2):
+                            head = 2 * (b * BANK_HEAD_PAIRS + u) + i
                             nc.tensor.transpose(
-                                xt[:, u, i, :],
-                                x_words[step][:, 2 * (a0 + u) + i, pair_words],
-                                ident[:],
+                                xt[:, u, i, :], x_words[step][:, head, pair_words], ident[:]
                             )
-                    nc.scalar.copy(
-                        out=grouped_words[:, q, a0 : a0 + 2, :, :],
-                        in_=xt[:].rearrange("p u i c -> p u c i"),
-                    )
-                width = HEAD_PAIRS * P * PACK
-                nc.vector.quantize_mx(
-                    out=x_codes[:, q].rearrange("p a c -> p (a c)").bitcast(FP8X4),
-                    scales=x_scales[:, q].rearrange("p a c -> p (a c)"),
-                    in_=grouped[:, q * width : (q + 1) * width],
-                )
+                    xt_banks[step, q, b] = xt
 
-            y_ps = psum_y.tile([P, STEP_T, D], F32)
+        def copy_out_and_quantise(step, q):
+            if q == 0:
+                grouped[step] = quant.tile(
+                    [P, PAIRS * HEAD_PAIRS * P * PACK], BF16, align_bytes=64, name="grouped"
+                )
+                x_codes[step] = quant.tile(
+                    [P, PAIRS, HEAD_PAIRS, P], U32, align_bytes=64, name="x_codes"
+                )
+                x_scales[step] = quant.tile(
+                    [P, PAIRS, HEAD_PAIRS, P], U8, align_bytes=64, name="x_scales"
+                )
+            grouped_words = grouped[step][:].bitcast(F32).rearrange(
+                "p (q a c i) -> p q a c i", q=PAIRS, a=HEAD_PAIRS, i=2
+            )
+            for b in range(HEAD_PAIRS // BANK_HEAD_PAIRS):
+                nc.scalar.copy(
+                    out=grouped_words[:, q, b * BANK_HEAD_PAIRS : (b + 1) * BANK_HEAD_PAIRS, :, :],
+                    in_=xt_banks[step, q, b][:].rearrange("p u i c -> p u c i"),
+                )
+            width = HEAD_PAIRS * P * PACK
+            nc.vector.quantize_mx(
+                out=x_codes[step][:, q].rearrange("p a c -> p (a c)").bitcast(FP8X4),
+                scales=x_scales[step][:, q].rearrange("p a c -> p (a c)"),
+                in_=grouped[step][:, q * width : (q + 1) * width],
+            )
+
+        def mx_passes(step):
+            y_ps[step] = psum_y.tile([P, STEP_T, D], F32, name="y_ps")
             for q in range(PAIRS):
                 for a in range(HEAD_PAIRS):
                     nc.tensor.matmul_mx(
-                        out=y_ps[:, q * PAIR_T : (q + 1) * PAIR_T, :].rearrange("p t f -> p (t f)"),
-                        lhsT=x_codes[:, q, a, :].bitcast(FP8X4),
-                        lhsT_scale=x_scales[:, q, a, :],
+                        out=y_ps[step][:, q * PAIR_T : (q + 1) * PAIR_T, :].rearrange(
+                            "p t f -> p (t f)"
+                        ),
+                        lhsT=x_codes[step][:, q, a, :].bitcast(FP8X4),
+                        lhsT_scale=x_scales[step][:, q, a, :],
                         rhs=w_codes[:, a, :].bitcast(FP8X4),
                         rhs_scale=w_scales[:, a, :],
                         start=(a == 0),
                         stop=(a == HEAD_PAIRS - 1),
                     )
 
-            res_bias = work.tile([P, STEP_T, D], F32)
+        def add_bias_to_residual(step):
+            res_bias[step] = work.tile([P, STEP_T, D], F32, name="res_bias")
             nc.vector.tensor_tensor(
-                out=res_bias[:],
+                out=res_bias[step][:],
                 in0=res_rows[step],
                 in1=bias_bc[:].unsqueeze(1).to_broadcast([P, STEP_T, D]),
                 op=ALU.add,
             )
 
-            y = work.tile([P, STEP_T, D], F32)
-            y_sum = stats.tile([P, STEP_T], F32)
+        def add_residual(step):
+            y[step] = work.tile([P, STEP_T, D], F32, name="y")
+            y_sum[step] = stats.tile([P, STEP_T], F32, name="y_sum")
             for t in range(STEP_T):
                 nc.vector.scalar_tensor_tensor(
-                    out=y[:, t, :],
-                    in0=y_ps[:, t, :],
+                    out=y[step][:, t, :],
+                    in0=y_ps[step][:, t, :],
                     scalar=1.0,
-                    in1=res_bias[:, t, :],
+                    in1=res_bias[step][:, t, :],
                     op0=ALU.mult,
                     op1=ALU.add,
-                    accum_out=y_sum[:, t : t + 1],
+                    accum_out=y_sum[step][:, t : t + 1],
                 )
-            mean = stats.tile([P, STEP_T], F32)
-            nc.vector.tensor_scalar_mul(out=mean[:], in0=y_sum[:], scalar1=1.0 / D)
 
-            squares = work.tile([P, STEP_T, D], BF16)
-            sq_sum = stats.tile([P, STEP_T], F32)
+        def mean_and_rstd(step):
+            mean[step] = stats.tile([P, STEP_T], F32, name="mean")
+            nc.scalar.mul(out=mean[step][:], in_=y_sum[step][:], mul=1.0 / D)
+            squares = work.tile([P, STEP_T, D], BF16, name="squares")
+            sq_sum = stats.tile([P, STEP_T], F32, name="sq_sum")
             for t in range(STEP_T):
                 nc.scalar.activation(
                     out=squares[:, t, :],
-                    in_=y[:, t, :],
+                    in_=y[step][:, t, :],
                     func=ACT.Square,
-                    bias=mean[:, t : t + 1],
+                    bias=mean[step][:, t : t + 1],
                     scale=-1.0,
                     accum_out=sq_sum[:, t : t + 1],
                 )
-            std = stats.tile([P, STEP_T], F32)
+            rstd[step] = stats.tile([P, STEP_T], F32, name="rstd")
             nc.scalar.activation(
-                out=std[:], in_=sq_sum[:], func=ACT.Sqrt, bias=eps[:], scale=1.0 / D
+                out=rstd[step][:],
+                in_=sq_sum[:],
+                func=ACT.Abs_reciprocal_sqrt,
+                bias=eps[:],
+                scale=1.0 / D,
             )
-            rstd = stats.tile([P, STEP_T], F32)
-            nc.vector.reciprocal(out=rstd[:], in_=std[:])
 
-            centred = work.tile([P, STEP_T, D], F32)
-            result = work.tile([P, STEP_T, D], F32)
+        def centre(step):
+            centred[step] = work.tile([P, STEP_T, D], F32, name="centred")
             for t in range(STEP_T):
                 nc.vector.scalar_tensor_tensor(
-                    out=centred[:, t, :],
-                    in0=y[:, t, :],
-                    scalar=mean[:, t : t + 1],
+                    out=centred[step][:, t, :],
+                    in0=y[step][:, t, :],
+                    scalar=mean[step][:, t : t + 1],
                     in1=gain_bc[:],
                     op0=ALU.subtract,
                     op1=ALU.mult,
                 )
+
+        def scale_shift_store(step):
+            result = results.tile([P, STEP_T, D], F32, name="result")
             for t in range(STEP_T):
                 nc.vector.scalar_tensor_tensor(
                     out=result[:, t, :],
-                    in0=centred[:, t, :],
-                    scalar=rstd[:, t : t + 1],
+                    in0=centred[step][:, t, :],
+                    scalar=rstd[step][:, t : t + 1],
                     in1=shift_bc[:],
                     op0=ALU.mult,
                     op1=ALU.add,
                 )
-            nc.sync.dma_start(
+            nc.gpsimd.dma_start(
                 out=out_dram[:, step * STEP_T : (step + 1) * STEP_T, :], in_=result[:]
             )
+
+        transposes(0)
+        for turn in range(STEPS + 2):
+            new, mid, old = turn, turn - 1, turn - 2
+            if new < STEPS:
+                add_bias_to_residual(new)
+            if 0 <= mid < STEPS:
+                add_residual(mid)
+            if new < STEPS:
+                copy_out_and_quantise(new, 0)
+            if new + 1 < STEPS:
+                transposes(new + 1)
+            if 0 <= old:
+                scale_shift_store(old)
+            if new < STEPS:
+                copy_out_and_quantise(new, 1)
+                mx_passes(new)
+            if 0 <= mid < STEPS:
+                mean_and_rstd(mid)
+                centre(mid)

@@ -83,17 +83,29 @@ def tile_multiheadattention_pb_t_kernel(
                 ),
                 in_=proj_w.rearrange("(h w e) f -> w h (e f)", h=HEADS, e=2),
             )
-        bias_bc = consts.tile([P, D], BF16)
-        gain_bc = consts.tile([P, D], BF16)
-        shift_bc = consts.tile([P, D], BF16)
-        nc.scalar.dma_start(out=bias_bc[:], in_=proj_b.partition_broadcast(P))
-        nc.scalar.dma_start(out=gain_bc[:], in_=ln_g.partition_broadcast(P))
-        nc.scalar.dma_start(out=shift_bc[:], in_=ln_b.partition_broadcast(P))
+        vec_rows = consts.tile([P, STEP_T, D], BF16)
+        nc.vector.memset(vec_rows[:], 0.0)
+        for n, vec in enumerate((proj_b, ln_g, ln_b)):
+            nc.scalar.dma_start(out=vec_rows[0:1, n, :], in_=vec.unsqueeze(0))
 
         ident = consts.tile([P, P], F32)
         make_identity(nc, ident[:])
         eps = consts.tile([P, 1], F32)
         nc.vector.memset(eps[:], LN_EPS)
+
+        ones = consts.tile([P, P], BF16)
+        nc.vector.memset(ones[:], 1.0)
+        spread_ps = psum_y.tile([P, STEP_T, D], F32, tag="y_ps", name="spread_ps")
+        nc.tensor.matmul(
+            out=spread_ps[:].rearrange("p n f -> p (n f)"),
+            lhsT=ones[:],
+            rhs=vec_rows[:].rearrange("p n f -> p (n f)"),
+            start=True,
+            stop=True,
+        )
+        spread = consts.tile([P, STEP_T, D], F32)
+        nc.vector.tensor_copy(out=spread[:], in_=spread_ps[:])
+        bias_bc, gain_bc, shift_bc = spread[:, 0, :], spread[:, 1, :], spread[:, 2, :]
 
         w_grouped = consts.tile([P, HEAD_PAIRS, PAIR_T, D, PACK], BF16, align_bytes=64)
         nc.vector.memset(w_grouped[:], 0.0)
@@ -175,7 +187,7 @@ def tile_multiheadattention_pb_t_kernel(
             nc.vector.tensor_tensor(
                 out=res_bias[step][:],
                 in0=res_rows[step],
-                in1=bias_bc[:].unsqueeze(1).to_broadcast([P, STEP_T, D]),
+                in1=bias_bc.unsqueeze(1).to_broadcast([P, STEP_T, D]),
                 op=ALU.add,
             )
 
@@ -223,7 +235,7 @@ def tile_multiheadattention_pb_t_kernel(
                     out=centred[step][:, t, :],
                     in0=y[step][:, t, :],
                     scalar=mean[step][:, t : t + 1],
-                    in1=gain_bc[:],
+                    in1=gain_bc,
                     op0=ALU.subtract,
                     op1=ALU.mult,
                 )
@@ -235,7 +247,7 @@ def tile_multiheadattention_pb_t_kernel(
                     out=result[:, t, :],
                     in0=centred[step][:, t, :],
                     scalar=rstd[step][:, t : t + 1],
-                    in1=shift_bc[:],
+                    in1=shift_bc,
                     op0=ALU.mult,
                     op1=ALU.add,
                 )

@@ -25,15 +25,17 @@ WORDS = DV // 2
 HEAD_PAIRS = HEADS // 2
 PACK = 4
 PAIR_T = 2
-STEP_T = 4
-PAIRS = STEP_T // PAIR_T
-STEPS = T_ALL // STEP_T
+N_PAIRS = T_ALL // PAIR_T
 BANK_HEAD_PAIRS = 2
-MAX_CHUNK_T = 16
+PAIR_BANKS = HEAD_PAIRS // BANK_HEAD_PAIRS
+FIRST_CHUNK_T = 4
+MAX_CHUNK_T = 8
+STORE_PAIRS = 2
+LAST_LAG = 6
 
 
 def chunk_sizes():
-    sizes = [STEP_T]
+    sizes = [FIRST_CHUNK_T]
     while sum(sizes) < T_ALL:
         sizes.append(min(sum(sizes), MAX_CHUNK_T))
     return sizes
@@ -50,10 +52,10 @@ def tile_multiheadattention_pb_t_kernel(
     with ExitStack() as ctx:
         consts = ctx.enter_context(tc.tile_pool(name="consts", bufs=1))
         loads = ctx.enter_context(tc.tile_pool(name="loads", bufs=1))
-        quant = ctx.enter_context(tc.tile_pool(name="quant", bufs=2))
-        work = ctx.enter_context(tc.tile_pool(name="work", bufs=2))
-        stats = ctx.enter_context(tc.tile_pool(name="stats", bufs=3))
-        results = ctx.enter_context(tc.tile_pool(name="results", bufs=12))
+        quant = ctx.enter_context(tc.tile_pool(name="quant", bufs=3))
+        work = ctx.enter_context(tc.tile_pool(name="work", bufs=4))
+        stats = ctx.enter_context(tc.tile_pool(name="stats", bufs=4))
+        results = ctx.enter_context(tc.tile_pool(name="results", bufs=10))
         psum_t = ctx.enter_context(tc.psum_pool(name="psum_t", bufs=6))
         psum_y = ctx.enter_context(tc.psum_pool(name="psum_y", bufs=2))
         ctx.enter_context(tc.manual_schedule())
@@ -70,9 +72,9 @@ def tile_multiheadattention_pb_t_kernel(
             res_sb = loads.tile([P, chunk_t, D], BF16, name="res%d" % c)
             nc.sync.dma_start(out=res_sb[:], in_=res_dram[:, t0 : t0 + chunk_t, :])
             chunk_words = x_sb[:].bitcast(F32).rearrange("p (h w) -> p h w", h=HEADS)
-            for s in range(chunk_t // STEP_T):
-                x_words.append(chunk_words[:, :, s * STEP_T * WORDS : (s + 1) * STEP_T * WORDS])
-                res_rows.append(res_sb[:, s * STEP_T : (s + 1) * STEP_T, :])
+            for s in range(chunk_t // PAIR_T):
+                x_words.append(chunk_words[:, :, s * PAIR_T * WORDS : (s + 1) * PAIR_T * WORDS])
+                res_rows.append(res_sb[:, s * PAIR_T : (s + 1) * PAIR_T, :])
             t0 += chunk_t
 
         w_rows = consts.tile([P, HEAD_PAIRS, PACK, D], BF16)
@@ -83,29 +85,17 @@ def tile_multiheadattention_pb_t_kernel(
                 ),
                 in_=proj_w.rearrange("(h w e) f -> w h (e f)", h=HEADS, e=2),
             )
-        vec_rows = consts.tile([P, STEP_T, D], BF16)
-        nc.vector.memset(vec_rows[:], 0.0)
-        for n, vec in enumerate((proj_b, ln_g, ln_b)):
-            nc.scalar.dma_start(out=vec_rows[0:1, n, :], in_=vec.unsqueeze(0))
+        bias_bc = consts.tile([P, D], BF16)
+        gain_bc = consts.tile([P, D], BF16)
+        shift_bc = consts.tile([P, D], BF16)
+        nc.scalar.dma_start(out=bias_bc[:], in_=proj_b.partition_broadcast(P))
+        nc.scalar.dma_start(out=gain_bc[:], in_=ln_g.partition_broadcast(P))
+        nc.scalar.dma_start(out=shift_bc[:], in_=ln_b.partition_broadcast(P))
 
         ident = consts.tile([P, P], F32)
         make_identity(nc, ident[:])
         eps = consts.tile([P, 1], F32)
         nc.vector.memset(eps[:], LN_EPS)
-
-        ones = consts.tile([P, P], BF16)
-        nc.vector.memset(ones[:], 1.0)
-        spread_ps = psum_y.tile([P, STEP_T, D], F32, tag="y_ps", name="spread_ps")
-        nc.tensor.matmul(
-            out=spread_ps[:].rearrange("p n f -> p (n f)"),
-            lhsT=ones[:],
-            rhs=vec_rows[:].rearrange("p n f -> p (n f)"),
-            start=True,
-            stop=True,
-        )
-        spread = consts.tile([P, STEP_T, D], F32)
-        nc.vector.tensor_copy(out=spread[:], in_=spread_ps[:])
-        bias_bc, gain_bc, shift_bc = spread[:, 0, :], spread[:, 1, :], spread[:, 2, :]
 
         w_grouped = consts.tile([P, HEAD_PAIRS, PAIR_T, D, PACK], BF16, align_bytes=64)
         nc.vector.memset(w_grouped[:], 0.0)
@@ -125,152 +115,144 @@ def tile_multiheadattention_pb_t_kernel(
         )
 
         xt_banks, grouped, x_codes, x_scales, y_ps = {}, {}, {}, {}, {}
-        res_bias, y, y_sum, mean, rstd, centred = {}, {}, {}, {}, {}, {}
+        res_bias, y, y_sum, mean, sq_sum, rstd, centred, result = {}, {}, {}, {}, {}, {}, {}, {}
 
-        def transposes(step):
-            for q in range(PAIRS):
-                pair_words = slice(q * PAIR_T * WORDS, (q + 1) * PAIR_T * WORDS)
-                for b in range(HEAD_PAIRS // BANK_HEAD_PAIRS):
-                    xt = psum_t.tile([P, BANK_HEAD_PAIRS, 2, P], F32, name="xt")
-                    for u in range(BANK_HEAD_PAIRS):
-                        for i in range(2):
-                            head = 2 * (b * BANK_HEAD_PAIRS + u) + i
-                            nc.tensor.transpose(
-                                xt[:, u, i, :], x_words[step][:, head, pair_words], ident[:]
-                            )
-                    xt_banks[step, q, b] = xt
+        def transposes(j):
+            for b in range(PAIR_BANKS):
+                xt = psum_t.tile([P, BANK_HEAD_PAIRS, 2, P], F32, name="xt")
+                for u in range(BANK_HEAD_PAIRS):
+                    for i in range(2):
+                        head = 2 * (b * BANK_HEAD_PAIRS + u) + i
+                        nc.tensor.transpose(xt[:, u, i, :], x_words[j][:, head, :], ident[:])
+                xt_banks[j, b] = xt
 
-        def copy_out_and_quantise(step, q):
-            if q == 0:
-                grouped[step] = quant.tile(
-                    [P, PAIRS * HEAD_PAIRS * P * PACK], BF16, align_bytes=64, name="grouped"
-                )
-                x_codes[step] = quant.tile(
-                    [P, PAIRS, HEAD_PAIRS, P], U32, align_bytes=64, name="x_codes"
-                )
-                x_scales[step] = quant.tile(
-                    [P, PAIRS, HEAD_PAIRS, P], U8, align_bytes=64, name="x_scales"
-                )
-            grouped_words = grouped[step][:].bitcast(F32).rearrange(
-                "p (q a c i) -> p q a c i", q=PAIRS, a=HEAD_PAIRS, i=2
+        def copy_out(j):
+            grouped[j] = quant.tile([P, HEAD_PAIRS * P * PACK], BF16, align_bytes=64, name="grouped")
+            grouped_words = grouped[j][:].bitcast(F32).rearrange(
+                "p (a c i) -> p a c i", a=HEAD_PAIRS, i=2
             )
-            for b in range(HEAD_PAIRS // BANK_HEAD_PAIRS):
+            for b in range(PAIR_BANKS):
                 nc.scalar.copy(
-                    out=grouped_words[:, q, b * BANK_HEAD_PAIRS : (b + 1) * BANK_HEAD_PAIRS, :, :],
-                    in_=xt_banks[step, q, b][:].rearrange("p u i c -> p u c i"),
+                    out=grouped_words[:, b * BANK_HEAD_PAIRS : (b + 1) * BANK_HEAD_PAIRS, :, :],
+                    in_=xt_banks[j, b][:].rearrange("p u i c -> p u c i"),
                 )
-            width = HEAD_PAIRS * P * PACK
+
+        def quantise(j):
+            x_codes[j] = quant.tile([P, HEAD_PAIRS, P], U32, align_bytes=64, name="x_codes")
+            x_scales[j] = quant.tile([P, HEAD_PAIRS, P], U8, align_bytes=64, name="x_scales")
             nc.vector.quantize_mx(
-                out=x_codes[step][:, q].rearrange("p a c -> p (a c)").bitcast(FP8X4),
-                scales=x_scales[step][:, q].rearrange("p a c -> p (a c)"),
-                in_=grouped[step][:, q * width : (q + 1) * width],
+                out=x_codes[j][:].rearrange("p a c -> p (a c)").bitcast(FP8X4),
+                scales=x_scales[j][:].rearrange("p a c -> p (a c)"),
+                in_=grouped[j][:],
             )
 
-        def mx_passes(step):
-            y_ps[step] = psum_y.tile([P, STEP_T, D], F32, name="y_ps")
-            for q in range(PAIRS):
-                for a in range(HEAD_PAIRS):
-                    nc.tensor.matmul_mx(
-                        out=y_ps[step][:, q * PAIR_T : (q + 1) * PAIR_T, :].rearrange(
-                            "p t f -> p (t f)"
-                        ),
-                        lhsT=x_codes[step][:, q, a, :].bitcast(FP8X4),
-                        lhsT_scale=x_scales[step][:, q, a, :],
-                        rhs=w_codes[:, a, :].bitcast(FP8X4),
-                        rhs_scale=w_scales[:, a, :],
-                        start=(a == 0),
-                        stop=(a == HEAD_PAIRS - 1),
-                    )
+        def mx_passes(j):
+            y_ps[j] = psum_y.tile([P, PAIR_T, D], F32, name="y_ps")
+            for a in range(HEAD_PAIRS):
+                nc.tensor.matmul_mx(
+                    out=y_ps[j][:].rearrange("p t f -> p (t f)"),
+                    lhsT=x_codes[j][:, a, :].bitcast(FP8X4),
+                    lhsT_scale=x_scales[j][:, a, :],
+                    rhs=w_codes[:, a, :].bitcast(FP8X4),
+                    rhs_scale=w_scales[:, a, :],
+                    start=(a == 0),
+                    stop=(a == HEAD_PAIRS - 1),
+                )
 
-        def add_bias_to_residual(step):
-            res_bias[step] = work.tile([P, STEP_T, D], F32, name="res_bias")
+        def add_bias_to_residual(j):
+            res_bias[j] = work.tile([P, PAIR_T, D], F32, name="res_bias")
             nc.vector.tensor_tensor(
-                out=res_bias[step][:],
-                in0=res_rows[step],
-                in1=bias_bc.unsqueeze(1).to_broadcast([P, STEP_T, D]),
+                out=res_bias[j][:],
+                in0=res_rows[j],
+                in1=bias_bc[:].unsqueeze(1).to_broadcast([P, PAIR_T, D]),
                 op=ALU.add,
             )
 
-        def add_residual(step):
-            y[step] = work.tile([P, STEP_T, D], F32, name="y")
-            y_sum[step] = stats.tile([P, STEP_T], F32, name="y_sum")
-            for t in range(STEP_T):
+        def add_residual(j):
+            y[j] = work.tile([P, PAIR_T, D], F32, name="y")
+            y_sum[j] = stats.tile([P, PAIR_T], F32, name="y_sum")
+            for t in range(PAIR_T):
                 nc.vector.scalar_tensor_tensor(
-                    out=y[step][:, t, :],
-                    in0=y_ps[step][:, t, :],
+                    out=y[j][:, t, :],
+                    in0=y_ps[j][:, t, :],
                     scalar=1.0,
-                    in1=res_bias[step][:, t, :],
+                    in1=res_bias[j][:, t, :],
                     op0=ALU.mult,
                     op1=ALU.add,
-                    accum_out=y_sum[step][:, t : t + 1],
+                    accum_out=y_sum[j][:, t : t + 1],
                 )
 
-        def mean_and_rstd(step):
-            mean[step] = stats.tile([P, STEP_T], F32, name="mean")
-            nc.scalar.mul(out=mean[step][:], in_=y_sum[step][:], mul=1.0 / D)
-            squares = work.tile([P, STEP_T, D], BF16, name="squares")
-            sq_sum = stats.tile([P, STEP_T], F32, name="sq_sum")
-            for t in range(STEP_T):
+        def mean_of(j):
+            mean[j] = stats.tile([P, PAIR_T], F32, name="mean")
+            nc.scalar.mul(out=mean[j][:], in_=y_sum[j][:], mul=1.0 / D)
+
+        def sum_squares(j):
+            squares = work.tile([P, PAIR_T, D], BF16, name="squares")
+            sq_sum[j] = stats.tile([P, PAIR_T], F32, name="sq_sum")
+            for t in range(PAIR_T):
                 nc.scalar.activation(
                     out=squares[:, t, :],
-                    in_=y[step][:, t, :],
+                    in_=y[j][:, t, :],
                     func=ACT.Square,
-                    bias=mean[step][:, t : t + 1],
+                    bias=mean[j][:, t : t + 1],
                     scale=-1.0,
-                    accum_out=sq_sum[:, t : t + 1],
+                    accum_out=sq_sum[j][:, t : t + 1],
                 )
-            rstd[step] = stats.tile([P, STEP_T], F32, name="rstd")
+
+        def rstd_of(j):
+            rstd[j] = stats.tile([P, PAIR_T], F32, name="rstd")
             nc.scalar.activation(
-                out=rstd[step][:],
-                in_=sq_sum[:],
+                out=rstd[j][:],
+                in_=sq_sum[j][:],
                 func=ACT.Abs_reciprocal_sqrt,
                 bias=eps[:],
                 scale=1.0 / D,
             )
 
-        def centre(step):
-            centred[step] = work.tile([P, STEP_T, D], F32, name="centred")
-            for t in range(STEP_T):
+        def centre(j):
+            centred[j] = work.tile([P, PAIR_T, D], F32, name="centred")
+            for t in range(PAIR_T):
                 nc.vector.scalar_tensor_tensor(
-                    out=centred[step][:, t, :],
-                    in0=y[step][:, t, :],
-                    scalar=mean[step][:, t : t + 1],
-                    in1=gain_bc,
+                    out=centred[j][:, t, :],
+                    in0=y[j][:, t, :],
+                    scalar=mean[j][:, t : t + 1],
+                    in1=gain_bc[:],
                     op0=ALU.subtract,
                     op1=ALU.mult,
                 )
 
-        def scale_shift_store(step):
-            result = results.tile([P, STEP_T, D], F32, name="result")
-            for t in range(STEP_T):
+        def scale_shift_store(j):
+            first = j - j % STORE_PAIRS
+            if j == first:
+                result[first] = results.tile([P, STORE_PAIRS * PAIR_T, D], F32, name="result")
+            for t in range(PAIR_T):
                 nc.vector.scalar_tensor_tensor(
-                    out=result[:, t, :],
-                    in0=centred[step][:, t, :],
-                    scalar=rstd[step][:, t : t + 1],
-                    in1=shift_bc,
+                    out=result[first][:, (j - first) * PAIR_T + t, :],
+                    in0=centred[j][:, t, :],
+                    scalar=rstd[j][:, t : t + 1],
+                    in1=shift_bc[:],
                     op0=ALU.mult,
                     op1=ALU.add,
                 )
-            nc.gpsimd.dma_start(
-                out=out_dram[:, step * STEP_T : (step + 1) * STEP_T, :], in_=result[:]
-            )
+            if j == first + STORE_PAIRS - 1:
+                nc.gpsimd.dma_start(
+                    out=out_dram[:, first * PAIR_T : (j + 1) * PAIR_T, :], in_=result[first][:]
+                )
+
+        def run(stage, j):
+            if 0 <= j < N_PAIRS:
+                stage(j)
 
         transposes(0)
-        for turn in range(STEPS + 2):
-            new, mid, old = turn, turn - 1, turn - 2
-            if new < STEPS:
-                add_bias_to_residual(new)
-            if 0 <= mid < STEPS:
-                add_residual(mid)
-            if new < STEPS:
-                copy_out_and_quantise(new, 0)
-            if new + 1 < STEPS:
-                transposes(new + 1)
-            if 0 <= old:
-                scale_shift_store(old)
-            if new < STEPS:
-                copy_out_and_quantise(new, 1)
-                mx_passes(new)
-            if 0 <= mid < STEPS:
-                mean_and_rstd(mid)
-                centre(mid)
+        for turn in range(N_PAIRS + LAST_LAG + 1):
+            run(transposes, turn + 1)
+            run(mx_passes, turn - 2)
+            run(mean_of, turn - 4)
+            run(rstd_of, turn - 5)
+            run(copy_out, turn)
+            run(sum_squares, turn - 4)
+            run(quantise, turn - 1)
+            run(add_residual, turn - 3)
+            run(centre, turn - 5)
+            run(scale_shift_store, turn - LAST_LAG)
+            run(add_bias_to_residual, turn - 2)

@@ -55,9 +55,10 @@ def tile_multiheadattention_pb_t_kernel(
         quant = ctx.enter_context(tc.tile_pool(name="quant", bufs=3))
         work = ctx.enter_context(tc.tile_pool(name="work", bufs=4))
         stats = ctx.enter_context(tc.tile_pool(name="stats", bufs=4))
-        results = ctx.enter_context(tc.tile_pool(name="results", bufs=10))
-        psum_t = ctx.enter_context(tc.psum_pool(name="psum_t", bufs=6))
+        results = ctx.enter_context(tc.tile_pool(name="results", bufs=N_PAIRS // STORE_PAIRS))
+        psum_t = ctx.enter_context(tc.psum_pool(name="psum_t", bufs=5))
         psum_y = ctx.enter_context(tc.psum_pool(name="psum_y", bufs=2))
+        psum_c = ctx.enter_context(tc.psum_pool(name="psum_c", bufs=1))
         ctx.enter_context(tc.manual_schedule())
 
         x_words = []
@@ -86,16 +87,19 @@ def tile_multiheadattention_pb_t_kernel(
                 in_=proj_w.rearrange("(h w e) f -> w h (e f)", h=HEADS, e=2),
             )
         bias_bc = consts.tile([P, D], BF16)
-        gain_bc = consts.tile([P, D], BF16)
-        shift_bc = consts.tile([P, D], BF16)
+        gain_shift = consts.tile([P, 2, D], BF16)
         nc.scalar.dma_start(out=bias_bc[:], in_=proj_b.partition_broadcast(P))
-        nc.scalar.dma_start(out=gain_bc[:], in_=ln_g.partition_broadcast(P))
-        nc.scalar.dma_start(out=shift_bc[:], in_=ln_b.partition_broadcast(P))
+        nc.scalar.dma_start(out=gain_shift[:, 0, :], in_=ln_g.partition_broadcast(P))
+        nc.scalar.dma_start(out=gain_shift[:, 1, :], in_=ln_b.partition_broadcast(P))
 
         ident = consts.tile([P, P], F32)
         make_identity(nc, ident[:])
         eps = consts.tile([P, 1], F32)
         nc.vector.memset(eps[:], LN_EPS)
+
+        averager = consts.tile([P, P], BF16)
+        nc.vector.memset(averager[:], 1.0 / P)
+        gain_shift_ps = psum_c.tile([P, 2, D], F32)
 
         w_grouped = consts.tile([P, HEAD_PAIRS, PAIR_T, D, PACK], BF16, align_bytes=64)
         nc.vector.memset(w_grouped[:], 0.0)
@@ -137,6 +141,15 @@ def tile_multiheadattention_pb_t_kernel(
                     in_=xt_banks[j, b][:].rearrange("p u i c -> p u c i"),
                 )
 
+        def spread_gain_shift():
+            nc.tensor.matmul(
+                gain_shift_ps[:].rearrange("p v f -> p (v f)"),
+                lhsT=averager[:],
+                rhs=gain_shift[:].rearrange("p v f -> p (v f)"),
+                start=True,
+                stop=True,
+            )
+
         def quantise(j):
             x_codes[j] = quant.tile([P, HEAD_PAIRS, P], U32, align_bytes=64, name="x_codes")
             x_scales[j] = quant.tile([P, HEAD_PAIRS, P], U8, align_bytes=64, name="x_scales")
@@ -161,7 +174,7 @@ def tile_multiheadattention_pb_t_kernel(
 
         def add_bias_to_residual(j):
             res_bias[j] = work.tile([P, PAIR_T, D], F32, name="res_bias")
-            nc.vector.tensor_tensor(
+            nc.gpsimd.tensor_tensor(
                 out=res_bias[j][:],
                 in0=res_rows[j],
                 in1=bias_bc[:].unsqueeze(1).to_broadcast([P, PAIR_T, D]),
@@ -216,7 +229,7 @@ def tile_multiheadattention_pb_t_kernel(
                     out=centred[j][:, t, :],
                     in0=y[j][:, t, :],
                     scalar=mean[j][:, t : t + 1],
-                    in1=gain_bc[:],
+                    in1=gain_shift_ps[:, 0, :],
                     op0=ALU.subtract,
                     op1=ALU.mult,
                 )
@@ -230,12 +243,12 @@ def tile_multiheadattention_pb_t_kernel(
                     out=result[first][:, (j - first) * PAIR_T + t, :],
                     in0=centred[j][:, t, :],
                     scalar=rstd[j][:, t : t + 1],
-                    in1=shift_bc[:],
+                    in1=gain_shift_ps[:, 1, :],
                     op0=ALU.mult,
                     op1=ALU.add,
                 )
             if j == first + STORE_PAIRS - 1:
-                nc.gpsimd.dma_start(
+                nc.sync.dma_start(
                     out=out_dram[:, first * PAIR_T : (j + 1) * PAIR_T, :], in_=result[first][:]
                 )
 
@@ -246,6 +259,8 @@ def tile_multiheadattention_pb_t_kernel(
         transposes(0)
         for turn in range(N_PAIRS + LAST_LAG + 1):
             run(transposes, turn + 1)
+            if turn == 2:
+                spread_gain_shift()
             run(mx_passes, turn - 2)
             run(mean_of, turn - 4)
             run(rstd_of, turn - 5)

@@ -31,7 +31,7 @@ PAIR_BANKS = HEAD_PAIRS // BANK_HEAD_PAIRS
 FIRST_CHUNK_T = 4
 MAX_CHUNK_T = 8
 STORE_PAIRS = 2
-LAST_LAG = 6
+LAST_LAG = 8
 
 
 def chunk_sizes():
@@ -53,9 +53,10 @@ def tile_multiheadattention_pb_t_kernel(
         consts = ctx.enter_context(tc.tile_pool(name="consts", bufs=1))
         loads = ctx.enter_context(tc.tile_pool(name="loads", bufs=1))
         quant = ctx.enter_context(tc.tile_pool(name="quant", bufs=3))
-        work = ctx.enter_context(tc.tile_pool(name="work", bufs=4))
-        stats = ctx.enter_context(tc.tile_pool(name="stats", bufs=4))
-        results = ctx.enter_context(tc.tile_pool(name="results", bufs=N_PAIRS // STORE_PAIRS))
+        work = ctx.enter_context(tc.tile_pool(name="work", bufs=5))
+        stats = ctx.enter_context(tc.tile_pool(name="stats", bufs=6))
+        biased = ctx.enter_context(tc.tile_pool(name="biased", bufs=3))
+        results = ctx.enter_context(tc.tile_pool(name="results", bufs=12))
         psum_t = ctx.enter_context(tc.psum_pool(name="psum_t", bufs=5))
         psum_y = ctx.enter_context(tc.psum_pool(name="psum_y", bufs=2))
         psum_c = ctx.enter_context(tc.psum_pool(name="psum_c", bufs=1))
@@ -119,7 +120,8 @@ def tile_multiheadattention_pb_t_kernel(
         )
 
         xt_banks, grouped, x_codes, x_scales, y_ps = {}, {}, {}, {}, {}
-        res_bias, y, y_sum, mean, sq_sum, rstd, centred, result = {}, {}, {}, {}, {}, {}, {}, {}
+        res_bias, y, y_sum, mean, sq_sum, rstd, result = {}, {}, {}, {}, {}, {}, {}
+        offset, normal, gained = {}, {}, {}
 
         def transposes(j):
             for b in range(PAIR_BANKS):
@@ -173,7 +175,7 @@ def tile_multiheadattention_pb_t_kernel(
                 )
 
         def add_bias_to_residual(j):
-            res_bias[j] = work.tile([P, PAIR_T, D], F32, name="res_bias")
+            res_bias[j] = biased.tile([P, PAIR_T, D], F32, name="res_bias")
             nc.gpsimd.tensor_tensor(
                 out=res_bias[j][:],
                 in0=res_rows[j],
@@ -197,7 +199,7 @@ def tile_multiheadattention_pb_t_kernel(
 
         def mean_of(j):
             mean[j] = stats.tile([P, PAIR_T], F32, name="mean")
-            nc.scalar.mul(out=mean[j][:], in_=y_sum[j][:], mul=1.0 / D)
+            nc.scalar.mul(out=mean[j][:], in_=y_sum[j][:], mul=-1.0 / D)
 
         def sum_squares(j):
             squares = work.tile([P, PAIR_T, D], BF16, name="squares")
@@ -208,7 +210,7 @@ def tile_multiheadattention_pb_t_kernel(
                     in_=y[j][:, t, :],
                     func=ACT.Square,
                     bias=mean[j][:, t : t + 1],
-                    scale=-1.0,
+                    scale=1.0,
                     accum_out=sq_sum[j][:, t : t + 1],
                 )
 
@@ -222,31 +224,40 @@ def tile_multiheadattention_pb_t_kernel(
                 scale=1.0 / D,
             )
 
-        def centre(j):
-            centred[j] = work.tile([P, PAIR_T, D], F32, name="centred")
+        def offset_of(j):
+            offset[j] = stats.tile([P, PAIR_T], F32, name="offset")
+            nc.gpsimd.tensor_tensor(out=offset[j][:], in0=mean[j][:], in1=rstd[j][:], op=ALU.mult)
+
+        def normalise(j):
+            normal[j] = work.tile([P, PAIR_T, D], F32, name="normal")
             for t in range(PAIR_T):
-                nc.vector.scalar_tensor_tensor(
-                    out=centred[j][:, t, :],
-                    in0=y[j][:, t, :],
-                    scalar=mean[j][:, t : t + 1],
-                    in1=gain_shift_ps[:, 0, :],
-                    op0=ALU.subtract,
-                    op1=ALU.mult,
+                nc.scalar.activation(
+                    out=normal[j][:, t, :],
+                    in_=y[j][:, t, :],
+                    func=ACT.Identity,
+                    bias=offset[j][:, t : t + 1],
+                    scale=rstd[j][:, t : t + 1],
                 )
 
-        def scale_shift_store(j):
+        def gain(j):
+            gained[j] = work.tile([P, PAIR_T, D], F32, name="gained")
+            nc.vector.tensor_tensor(
+                out=gained[j][:],
+                in0=normal[j][:],
+                in1=gain_shift_ps[:, 0, :].unsqueeze(1).to_broadcast([P, PAIR_T, D]),
+                op=ALU.mult,
+            )
+
+        def shift_store(j):
             first = j - j % STORE_PAIRS
             if j == first:
                 result[first] = results.tile([P, STORE_PAIRS * PAIR_T, D], F32, name="result")
-            for t in range(PAIR_T):
-                nc.vector.scalar_tensor_tensor(
-                    out=result[first][:, (j - first) * PAIR_T + t, :],
-                    in0=centred[j][:, t, :],
-                    scalar=rstd[j][:, t : t + 1],
-                    in1=gain_shift_ps[:, 1, :],
-                    op0=ALU.mult,
-                    op1=ALU.add,
-                )
+            nc.vector.tensor_tensor(
+                out=result[first][:, (j - first) * PAIR_T : (j - first + 1) * PAIR_T, :],
+                in0=gained[j][:],
+                in1=gain_shift_ps[:, 1, :].unsqueeze(1).to_broadcast([P, PAIR_T, D]),
+                op=ALU.add,
+            )
             if j == first + STORE_PAIRS - 1:
                 nc.sync.dma_start(
                     out=out_dram[:, first * PAIR_T : (j + 1) * PAIR_T, :], in_=result[first][:]
@@ -266,8 +277,10 @@ def tile_multiheadattention_pb_t_kernel(
             run(rstd_of, turn - 5)
             run(copy_out, turn)
             run(sum_squares, turn - 4)
+            run(normalise, turn - 6)
             run(quantise, turn - 1)
             run(add_residual, turn - 3)
-            run(centre, turn - 5)
-            run(scale_shift_store, turn - LAST_LAG)
+            run(shift_store, turn - LAST_LAG)
+            run(gain, turn - 7)
             run(add_bias_to_residual, turn - 2)
+            run(offset_of, turn - 5)

@@ -62,6 +62,26 @@ def tile_multiheadattention_pb_t_kernel(
         psum_c = ctx.enter_context(tc.psum_pool(name="psum_c", bufs=1))
         ctx.enter_context(tc.manual_schedule())
 
+        vectors = consts.tile([P, 3, D], BF16)
+        nc.vector.memset(vectors[:], 0.0)
+        for v, vector in enumerate((ln_g, ln_b, proj_b)):
+            nc.scalar.dma_start(out=vectors[0:1, v, :], in_=vector.unsqueeze(0))
+        ones = consts.tile([P, P], BF16)
+        nc.vector.memset(ones[:], 1.0)
+        ident = consts.tile([P, P], F32)
+        make_identity(nc, ident[:])
+
+        w_rows = consts.tile([P, HEAD_PAIRS, PACK, D], BF16)
+
+        def load_weights():
+            for s in range(PAIR_T):
+                nc.sync.dma_start(
+                    out=w_rows[s * WORDS : (s + 1) * WORDS].rearrange(
+                        "p a (i e) f -> p (a i) (e f)", i=2
+                    ),
+                    in_=proj_w.rearrange("(h w e) f -> w h (e f)", h=HEADS, e=2),
+                )
+
         x_words = []
         res_rows = []
         t0 = 0
@@ -71,6 +91,8 @@ def tile_multiheadattention_pb_t_kernel(
                 out=x_sb[:].rearrange("p (h t j) -> p h t j", h=HEADS, t=chunk_t),
                 in_=x_dram[:, :, t0 : t0 + chunk_t, :],
             )
+            if c == 0:
+                load_weights()
             res_sb = loads.tile([P, chunk_t, D], BF16, name="res%d" % c)
             nc.sync.dma_start(out=res_sb[:], in_=res_dram[:, t0 : t0 + chunk_t, :])
             chunk_words = x_sb[:].bitcast(F32).rearrange("p (h w) -> p h w", h=HEADS)
@@ -79,28 +101,18 @@ def tile_multiheadattention_pb_t_kernel(
                 res_rows.append(res_sb[:, s * PAIR_T : (s + 1) * PAIR_T, :])
             t0 += chunk_t
 
-        w_rows = consts.tile([P, HEAD_PAIRS, PACK, D], BF16)
-        for s in range(PAIR_T):
-            nc.scalar.dma_start(
-                out=w_rows[s * WORDS : (s + 1) * WORDS].rearrange(
-                    "p a (i e) f -> p (a i) (e f)", i=2
-                ),
-                in_=proj_w.rearrange("(h w e) f -> w h (e f)", h=HEADS, e=2),
-            )
+        vectors_ps = psum_c.tile([P, 3, D], F32)
+        nc.tensor.matmul(
+            vectors_ps[:].rearrange("p v f -> p (v f)"),
+            lhsT=ones[:],
+            rhs=vectors[:].rearrange("p v f -> p (v f)"),
+            start=True,
+            stop=True,
+        )
         bias_bc = consts.tile([P, D], BF16)
-        gain_shift = consts.tile([P, 2, D], BF16)
-        nc.scalar.dma_start(out=bias_bc[:], in_=proj_b.partition_broadcast(P))
-        nc.scalar.dma_start(out=gain_shift[:, 0, :], in_=ln_g.partition_broadcast(P))
-        nc.scalar.dma_start(out=gain_shift[:, 1, :], in_=ln_b.partition_broadcast(P))
-
-        ident = consts.tile([P, P], F32)
-        make_identity(nc, ident[:])
+        nc.scalar.copy(out=bias_bc[:], in_=vectors_ps[:, 2, :])
         eps = consts.tile([P, 1], F32)
         nc.vector.memset(eps[:], LN_EPS)
-
-        averager = consts.tile([P, P], BF16)
-        nc.vector.memset(averager[:], 1.0 / P)
-        gain_shift_ps = psum_c.tile([P, 2, D], F32)
 
         w_grouped = consts.tile([P, HEAD_PAIRS, PAIR_T, D, PACK], BF16, align_bytes=64)
         nc.vector.memset(w_grouped[:], 0.0)
@@ -142,15 +154,6 @@ def tile_multiheadattention_pb_t_kernel(
                     out=grouped_words[:, b * BANK_HEAD_PAIRS : (b + 1) * BANK_HEAD_PAIRS, :, :],
                     in_=xt_banks[j, b][:].rearrange("p u i c -> p u c i"),
                 )
-
-        def spread_gain_shift():
-            nc.tensor.matmul(
-                gain_shift_ps[:].rearrange("p v f -> p (v f)"),
-                lhsT=averager[:],
-                rhs=gain_shift[:].rearrange("p v f -> p (v f)"),
-                start=True,
-                stop=True,
-            )
 
         def quantise(j):
             x_codes[j] = quant.tile([P, HEAD_PAIRS, P], U32, align_bytes=64, name="x_codes")
@@ -244,7 +247,7 @@ def tile_multiheadattention_pb_t_kernel(
             nc.vector.tensor_tensor(
                 out=gained[j][:],
                 in0=normal[j][:],
-                in1=gain_shift_ps[:, 0, :].unsqueeze(1).to_broadcast([P, PAIR_T, D]),
+                in1=vectors_ps[:, 0, :].unsqueeze(1).to_broadcast([P, PAIR_T, D]),
                 op=ALU.mult,
             )
 
@@ -255,7 +258,7 @@ def tile_multiheadattention_pb_t_kernel(
             nc.vector.tensor_tensor(
                 out=result[first][:, (j - first) * PAIR_T : (j - first + 1) * PAIR_T, :],
                 in0=gained[j][:],
-                in1=gain_shift_ps[:, 1, :].unsqueeze(1).to_broadcast([P, PAIR_T, D]),
+                in1=vectors_ps[:, 1, :].unsqueeze(1).to_broadcast([P, PAIR_T, D]),
                 op=ALU.add,
             )
             if j == first + STORE_PAIRS - 1:
@@ -270,8 +273,6 @@ def tile_multiheadattention_pb_t_kernel(
         transposes(0)
         for turn in range(N_PAIRS + LAST_LAG + 1):
             run(transposes, turn + 1)
-            if turn == 2:
-                spread_gain_shift()
             run(mx_passes, turn - 2)
             run(mean_of, turn - 4)
             run(rstd_of, turn - 5)

@@ -28,10 +28,11 @@ PAIR_T = 2
 N_PAIRS = T_ALL // PAIR_T
 BANK_HEAD_PAIRS = 2
 PAIR_BANKS = HEAD_PAIRS // BANK_HEAD_PAIRS
-FIRST_CHUNK_T = 4
+FIRST_CHUNK_T = 2
 MAX_CHUNK_T = 8
+RES_CHUNK_T = 8
 STORE_PAIRS = 2
-LAST_LAG = 8
+LAST_LAG = 7
 
 
 def chunk_sizes():
@@ -82,6 +83,7 @@ def tile_multiheadattention_pb_t_kernel(
                     in_=proj_w.rearrange("(h w e) f -> w h (e f)", h=HEADS, e=2),
                 )
 
+        load_weights()
         x_words = []
         res_rows = []
         t0 = 0
@@ -91,49 +93,50 @@ def tile_multiheadattention_pb_t_kernel(
                 out=x_sb[:].rearrange("p (h t j) -> p h t j", h=HEADS, t=chunk_t),
                 in_=x_dram[:, :, t0 : t0 + chunk_t, :],
             )
-            if c == 0:
-                load_weights()
-            res_sb = loads.tile([P, chunk_t, D], BF16, name="res%d" % c)
-            nc.sync.dma_start(out=res_sb[:], in_=res_dram[:, t0 : t0 + chunk_t, :])
             chunk_words = x_sb[:].bitcast(F32).rearrange("p (h w) -> p h w", h=HEADS)
             for s in range(chunk_t // PAIR_T):
                 x_words.append(chunk_words[:, :, s * PAIR_T * WORDS : (s + 1) * PAIR_T * WORDS])
-                res_rows.append(res_sb[:, s * PAIR_T : (s + 1) * PAIR_T, :])
             t0 += chunk_t
+            r0 = len(res_rows) * PAIR_T
+            if 2 * (t0 - r0) >= RES_CHUNK_T:
+                res_sb = loads.tile([P, RES_CHUNK_T, D], BF16, name="res%d" % c)
+                nc.sync.dma_start(out=res_sb[:], in_=res_dram[:, r0 : r0 + RES_CHUNK_T, :])
+                for s in range(RES_CHUNK_T // PAIR_T):
+                    res_rows.append(res_sb[:, s * PAIR_T : (s + 1) * PAIR_T, :])
 
         vectors_ps = psum_c.tile([P, 3, D], F32)
-        nc.tensor.matmul(
-            vectors_ps[:].rearrange("p v f -> p (v f)"),
-            lhsT=ones[:],
-            rhs=vectors[:].rearrange("p v f -> p (v f)"),
-            start=True,
-            stop=True,
-        )
         bias_bc = consts.tile([P, D], BF16)
-        nc.scalar.copy(out=bias_bc[:], in_=vectors_ps[:, 2, :])
+
+        def spread_vectors():
+            nc.tensor.matmul(
+                vectors_ps[:].rearrange("p v f -> p (v f)"),
+                lhsT=ones[:],
+                rhs=vectors[:].rearrange("p v f -> p (v f)"),
+                start=True,
+                stop=True,
+            )
+
         eps = consts.tile([P, 1], F32)
         nc.vector.memset(eps[:], LN_EPS)
 
-        w_grouped = consts.tile([P, HEAD_PAIRS, PAIR_T, D, PACK], BF16, align_bytes=64)
+        w_grouped = consts.tile([P, HEAD_PAIRS, D, PAIR_T, PACK], BF16, align_bytes=64)
         nc.vector.memset(w_grouped[:], 0.0)
         lower, upper = slice(0, WORDS), slice(WORDS, P)
-        nc.vector.tensor_copy(
-            out=w_grouped[lower, :, 0, :, :], in_=w_rows[lower].rearrange("p a v f -> p a f v")
-        )
-        nc.scalar.copy(
-            out=w_grouped[upper, :, 1, :, :], in_=w_rows[upper].rearrange("p a v f -> p a f v")
-        )
+        w_spread = w_rows[:].rearrange("p a v f -> p a f v")
+        nc.vector.tensor_copy(out=w_grouped[lower, :, :, 0, :], in_=w_spread[lower])
+        nc.vector.tensor_copy(out=w_grouped[upper, 3:, :, 1, :], in_=w_spread[upper, 3:])
+        nc.scalar.copy(out=w_grouped[upper, :3, :, 1, :], in_=w_spread[upper, :3])
         w_codes = consts.tile([P, HEAD_PAIRS, PAIR_T * D], U32, align_bytes=64)
         w_scales = consts.tile([P, HEAD_PAIRS, PAIR_T * D], U8, align_bytes=64)
         nc.vector.quantize_mx(
             out=w_codes[:].rearrange("p a n -> p (a n)").bitcast(FP8X4),
             scales=w_scales[:].rearrange("p a n -> p (a n)"),
-            in_=w_grouped[:].rearrange("p a s f v -> p (a s f v)"),
+            in_=w_grouped[:].rearrange("p a f s v -> p (a f s v)"),
         )
 
         xt_banks, grouped, x_codes, x_scales, y_ps = {}, {}, {}, {}, {}
-        res_bias, y, y_sum, mean, sq_sum, rstd, result = {}, {}, {}, {}, {}, {}, {}
-        offset, normal, gained = {}, {}, {}
+        res_bias, y, stat, mean_neg, rstd, offset = {}, {}, {}, {}, {}, {}
+        normal, gained, result = {}, {}, {}
 
         def transposes(j):
             for b in range(PAIR_BANKS):
@@ -165,10 +168,10 @@ def tile_multiheadattention_pb_t_kernel(
             )
 
         def mx_passes(j):
-            y_ps[j] = psum_y.tile([P, PAIR_T, D], F32, name="y_ps")
+            y_ps[j] = psum_y.tile([P, D, PAIR_T], F32, name="y_ps")
             for a in range(HEAD_PAIRS):
                 nc.tensor.matmul_mx(
-                    out=y_ps[j][:].rearrange("p t f -> p (t f)"),
+                    out=y_ps[j][:].rearrange("p f t -> p (f t)"),
                     lhsT=x_codes[j][:, a, :].bitcast(FP8X4),
                     lhsT_scale=x_scales[j][:, a, :],
                     rhs=w_codes[:, a, :].bitcast(FP8X4),
@@ -178,65 +181,51 @@ def tile_multiheadattention_pb_t_kernel(
                 )
 
         def add_bias_to_residual(j):
-            res_bias[j] = biased.tile([P, PAIR_T, D], F32, name="res_bias")
+            res_bias[j] = biased.tile([P, D, PAIR_T], F32, name="res_bias")
             nc.gpsimd.tensor_tensor(
                 out=res_bias[j][:],
-                in0=res_rows[j],
-                in1=bias_bc[:].unsqueeze(1).to_broadcast([P, PAIR_T, D]),
+                in0=res_rows[j].rearrange("p t f -> p f t"),
+                in1=bias_bc[:].unsqueeze(2).to_broadcast([P, D, PAIR_T]),
                 op=ALU.add,
             )
 
         def add_residual(j):
-            y[j] = work.tile([P, PAIR_T, D], F32, name="y")
-            y_sum[j] = stats.tile([P, PAIR_T], F32, name="y_sum")
-            for t in range(PAIR_T):
-                nc.vector.scalar_tensor_tensor(
-                    out=y[j][:, t, :],
-                    in0=y_ps[j][:, t, :],
-                    scalar=1.0,
-                    in1=res_bias[j][:, t, :],
-                    op0=ALU.mult,
-                    op1=ALU.add,
-                    accum_out=y_sum[j][:, t : t + 1],
-                )
+            y[j] = work.tile([P, D, PAIR_T], F32, name="y")
+            nc.vector.tensor_tensor(out=y[j][:], in0=y_ps[j][:], in1=res_bias[j][:], op=ALU.add)
 
-        def mean_of(j):
-            mean[j] = stats.tile([P, PAIR_T], F32, name="mean")
-            nc.scalar.mul(out=mean[j][:], in_=y_sum[j][:], mul=-1.0 / D)
-
-        def sum_squares(j):
-            squares = work.tile([P, PAIR_T, D], BF16, name="squares")
-            sq_sum[j] = stats.tile([P, PAIR_T], F32, name="sq_sum")
-            for t in range(PAIR_T):
-                nc.scalar.activation(
-                    out=squares[:, t, :],
-                    in_=y[j][:, t, :],
-                    func=ACT.Square,
-                    bias=mean[j][:, t : t + 1],
-                    scale=1.0,
-                    accum_out=sq_sum[j][:, t : t + 1],
-                )
+        def statistics(j):
+            stat[j] = stats.tile([P, PAIR_T, 3], F32, name="stat")
+            nc.vector.bn_stats(
+                out=stat[j][:].rearrange("p t v -> p (t v)"),
+                in_=y[j][:].rearrange("p f t -> p (f t)"),
+            )
 
         def rstd_of(j):
             rstd[j] = stats.tile([P, PAIR_T], F32, name="rstd")
             nc.scalar.activation(
                 out=rstd[j][:],
-                in_=sq_sum[j][:],
+                in_=stat[j][:, :, 2],
                 func=ACT.Abs_reciprocal_sqrt,
                 bias=eps[:],
                 scale=1.0 / D,
             )
 
+        def mean_neg_of(j):
+            mean_neg[j] = stats.tile([P, PAIR_T], F32, name="mean_neg")
+            nc.scalar.mul(out=mean_neg[j][:], in_=stat[j][:, :, 1], mul=-1.0)
+
         def offset_of(j):
             offset[j] = stats.tile([P, PAIR_T], F32, name="offset")
-            nc.gpsimd.tensor_tensor(out=offset[j][:], in0=mean[j][:], in1=rstd[j][:], op=ALU.mult)
+            nc.gpsimd.tensor_tensor(
+                out=offset[j][:], in0=mean_neg[j][:], in1=rstd[j][:], op=ALU.mult
+            )
 
         def normalise(j):
             normal[j] = work.tile([P, PAIR_T, D], F32, name="normal")
             for t in range(PAIR_T):
                 nc.scalar.activation(
                     out=normal[j][:, t, :],
-                    in_=y[j][:, t, :],
+                    in_=y[j][:, :, t],
                     func=ACT.Identity,
                     bias=offset[j][:, t : t + 1],
                     scale=rstd[j][:, t : t + 1],
@@ -273,15 +262,19 @@ def tile_multiheadattention_pb_t_kernel(
         transposes(0)
         for turn in range(N_PAIRS + LAST_LAG + 1):
             run(transposes, turn + 1)
+            if turn == 0:
+                spread_vectors()
             run(mx_passes, turn - 2)
-            run(mean_of, turn - 4)
-            run(rstd_of, turn - 5)
+            run(rstd_of, turn - 4)
+            run(mean_neg_of, turn - 4)
             run(copy_out, turn)
-            run(sum_squares, turn - 4)
-            run(normalise, turn - 6)
+            if turn == 0:
+                nc.scalar.copy(out=bias_bc[:], in_=vectors_ps[:, 2, :])
+            run(normalise, turn - 5)
             run(quantise, turn - 1)
             run(add_residual, turn - 3)
             run(shift_store, turn - LAST_LAG)
-            run(gain, turn - 7)
+            run(statistics, turn - 3)
+            run(gain, turn - 6)
+            run(offset_of, turn - 4)
             run(add_bias_to_residual, turn - 2)
-            run(offset_of, turn - 5)

@@ -31,8 +31,10 @@ PAIR_BANKS = HEAD_PAIRS // BANK_HEAD_PAIRS
 FIRST_CHUNK_T = 2
 MAX_CHUNK_T = 8
 RES_CHUNK_T = 8
-STORE_PAIRS = 2
-LAST_LAG = 7
+QUAD = 2
+QUAD_T = QUAD * PAIR_T
+N_QUADS = N_PAIRS // QUAD
+LAST_LAG = 8
 
 
 def chunk_sizes():
@@ -54,9 +56,9 @@ def tile_multiheadattention_pb_t_kernel(
         consts = ctx.enter_context(tc.tile_pool(name="consts", bufs=1))
         loads = ctx.enter_context(tc.tile_pool(name="loads", bufs=1))
         quant = ctx.enter_context(tc.tile_pool(name="quant", bufs=3))
-        work = ctx.enter_context(tc.tile_pool(name="work", bufs=5))
-        stats = ctx.enter_context(tc.tile_pool(name="stats", bufs=6))
-        biased = ctx.enter_context(tc.tile_pool(name="biased", bufs=3))
+        work = ctx.enter_context(tc.tile_pool(name="work", bufs=3))
+        stats = ctx.enter_context(tc.tile_pool(name="stats", bufs=3))
+        biased = ctx.enter_context(tc.tile_pool(name="biased", bufs=2))
         results = ctx.enter_context(tc.tile_pool(name="results", bufs=12))
         psum_t = ctx.enter_context(tc.psum_pool(name="psum_t", bufs=5))
         psum_y = ctx.enter_context(tc.psum_pool(name="psum_y", bufs=2))
@@ -65,8 +67,6 @@ def tile_multiheadattention_pb_t_kernel(
 
         vectors = consts.tile([P, 3, D], BF16)
         nc.vector.memset(vectors[:], 0.0)
-        for v, vector in enumerate((ln_g, ln_b, proj_b)):
-            nc.scalar.dma_start(out=vectors[0:1, v, :], in_=vector.unsqueeze(0))
         ones = consts.tile([P, P], BF16)
         nc.vector.memset(ones[:], 1.0)
         ident = consts.tile([P, P], F32)
@@ -83,7 +83,6 @@ def tile_multiheadattention_pb_t_kernel(
                     in_=proj_w.rearrange("(h w e) f -> w h (e f)", h=HEADS, e=2),
                 )
 
-        load_weights()
         x_words = []
         res_rows = []
         t0 = 0
@@ -93,16 +92,20 @@ def tile_multiheadattention_pb_t_kernel(
                 out=x_sb[:].rearrange("p (h t j) -> p h t j", h=HEADS, t=chunk_t),
                 in_=x_dram[:, :, t0 : t0 + chunk_t, :],
             )
+            if c == 0:
+                load_weights()
+                for v, vector in enumerate((ln_g, ln_b, proj_b)):
+                    nc.sync.dma_start(out=vectors[0:1, v, :], in_=vector.unsqueeze(0))
             chunk_words = x_sb[:].bitcast(F32).rearrange("p (h w) -> p h w", h=HEADS)
             for s in range(chunk_t // PAIR_T):
                 x_words.append(chunk_words[:, :, s * PAIR_T * WORDS : (s + 1) * PAIR_T * WORDS])
             t0 += chunk_t
-            r0 = len(res_rows) * PAIR_T
+            r0 = len(res_rows) * QUAD_T
             if 2 * (t0 - r0) >= RES_CHUNK_T:
                 res_sb = loads.tile([P, RES_CHUNK_T, D], BF16, name="res%d" % c)
                 nc.sync.dma_start(out=res_sb[:], in_=res_dram[:, r0 : r0 + RES_CHUNK_T, :])
-                for s in range(RES_CHUNK_T // PAIR_T):
-                    res_rows.append(res_sb[:, s * PAIR_T : (s + 1) * PAIR_T, :])
+                for s in range(RES_CHUNK_T // QUAD_T):
+                    res_rows.append(res_sb[:, s * QUAD_T : (s + 1) * QUAD_T, :])
 
         vectors_ps = psum_c.tile([P, 3, D], F32)
         bias_bc = consts.tile([P, D], BF16)
@@ -124,19 +127,23 @@ def tile_multiheadattention_pb_t_kernel(
         lower, upper = slice(0, WORDS), slice(WORDS, P)
         w_spread = w_rows[:].rearrange("p a v f -> p a f v")
         nc.vector.tensor_copy(out=w_grouped[lower, :, :, 0, :], in_=w_spread[lower])
-        nc.vector.tensor_copy(out=w_grouped[upper, 3:, :, 1, :], in_=w_spread[upper, 3:])
-        nc.scalar.copy(out=w_grouped[upper, :3, :, 1, :], in_=w_spread[upper, :3])
+
+        def lay_out_upper():
+            nc.scalar.copy(out=w_grouped[upper, :, :, 1, :], in_=w_spread[upper])
+
         w_codes = consts.tile([P, HEAD_PAIRS, PAIR_T * D], U32, align_bytes=64)
         w_scales = consts.tile([P, HEAD_PAIRS, PAIR_T * D], U8, align_bytes=64)
-        nc.vector.quantize_mx(
-            out=w_codes[:].rearrange("p a n -> p (a n)").bitcast(FP8X4),
-            scales=w_scales[:].rearrange("p a n -> p (a n)"),
-            in_=w_grouped[:].rearrange("p a f s v -> p (a f s v)"),
-        )
+
+        def quantise_weights():
+            nc.vector.quantize_mx(
+                out=w_codes[:].rearrange("p a n -> p (a n)").bitcast(FP8X4),
+                scales=w_scales[:].rearrange("p a n -> p (a n)"),
+                in_=w_grouped[:].rearrange("p a f s v -> p (a f s v)"),
+            )
 
         xt_banks, grouped, x_codes, x_scales, y_ps = {}, {}, {}, {}, {}
         res_bias, y, stat, mean_neg, rstd, offset = {}, {}, {}, {}, {}, {}
-        normal, gained, result = {}, {}, {}
+        normal, gained = {}, {}
 
         def transposes(j):
             for b in range(PAIR_BANKS):
@@ -168,113 +175,130 @@ def tile_multiheadattention_pb_t_kernel(
             )
 
         def mx_passes(j):
-            y_ps[j] = psum_y.tile([P, D, PAIR_T], F32, name="y_ps")
-            for a in range(HEAD_PAIRS):
+            q, h = divmod(j, QUAD)
+            if h == 0:
+                y_ps[q] = psum_y.tile([P, QUAD, D, PAIR_T], F32, name="y_ps")
+            for a, start, stop in ((0, True, True),) + tuple(
+                (a, a == 0, a == HEAD_PAIRS - 1) for a in range(HEAD_PAIRS)
+            ):
                 nc.tensor.matmul_mx(
-                    out=y_ps[j][:].rearrange("p f t -> p (f t)"),
+                    out=y_ps[q][:, h].rearrange("p f t -> p (f t)"),
                     lhsT=x_codes[j][:, a, :].bitcast(FP8X4),
                     lhsT_scale=x_scales[j][:, a, :],
                     rhs=w_codes[:, a, :].bitcast(FP8X4),
                     rhs_scale=w_scales[:, a, :],
-                    start=(a == 0),
-                    stop=(a == HEAD_PAIRS - 1),
+                    start=start,
+                    stop=stop,
                 )
 
-        def add_bias_to_residual(j):
-            res_bias[j] = biased.tile([P, D, PAIR_T], F32, name="res_bias")
+        def add_bias_to_residual(q):
+            res_bias[q] = biased.tile([P, QUAD, D, PAIR_T], F32, name="res_bias")
             nc.gpsimd.tensor_tensor(
-                out=res_bias[j][:],
-                in0=res_rows[j].rearrange("p t f -> p f t"),
-                in1=bias_bc[:].unsqueeze(2).to_broadcast([P, D, PAIR_T]),
+                out=res_bias[q][:],
+                in0=res_rows[q].rearrange("p (h t) f -> p h f t", h=QUAD),
+                in1=bias_bc[:].unsqueeze(1).unsqueeze(3).to_broadcast([P, QUAD, D, PAIR_T]),
                 op=ALU.add,
             )
 
-        def add_residual(j):
-            y[j] = work.tile([P, D, PAIR_T], F32, name="y")
-            nc.vector.tensor_tensor(out=y[j][:], in0=y_ps[j][:], in1=res_bias[j][:], op=ALU.add)
-
-        def statistics(j):
-            stat[j] = stats.tile([P, PAIR_T, 3], F32, name="stat")
-            nc.vector.bn_stats(
-                out=stat[j][:].rearrange("p t v -> p (t v)"),
-                in_=y[j][:].rearrange("p f t -> p (f t)"),
+        def add_residual(q):
+            y[q] = work.tile([P, QUAD, D, PAIR_T], F32, name="y")
+            nc.vector.tensor_tensor(
+                out=y[q][:],
+                in0=y_ps[q][:],
+                in1=res_bias[q][:],
+                op=ALU.add,
             )
 
-        def rstd_of(j):
-            rstd[j] = stats.tile([P, PAIR_T], F32, name="rstd")
+        def statistics(j):
+            q, h = divmod(j, QUAD)
+            if h == 0:
+                stat[q] = stats.tile([P, QUAD, PAIR_T, 3], F32, name="stat")
+            nc.vector.bn_stats(
+                out=stat[q][:, h].rearrange("p t v -> p (t v)"),
+                in_=y[q][:, h].rearrange("p f t -> p (f t)"),
+            )
+
+        def rstd_of(q):
+            rstd[q] = stats.tile([P, QUAD, PAIR_T], F32, name="rstd")
             nc.scalar.activation(
-                out=rstd[j][:],
-                in_=stat[j][:, :, 2],
+                out=rstd[q][:],
+                in_=stat[q][:, :, :, 2],
                 func=ACT.Abs_reciprocal_sqrt,
                 bias=eps[:],
                 scale=1.0 / D,
             )
+            mean_neg[q] = stats.tile([P, QUAD, PAIR_T], F32, name="mean_neg")
+            nc.scalar.mul(out=mean_neg[q][:], in_=stat[q][:, :, :, 1], mul=-1.0)
 
-        def mean_neg_of(j):
-            mean_neg[j] = stats.tile([P, PAIR_T], F32, name="mean_neg")
-            nc.scalar.mul(out=mean_neg[j][:], in_=stat[j][:, :, 1], mul=-1.0)
-
-        def offset_of(j):
-            offset[j] = stats.tile([P, PAIR_T], F32, name="offset")
+        def offset_of(q):
+            offset[q] = stats.tile([P, QUAD, PAIR_T], F32, name="offset")
             nc.gpsimd.tensor_tensor(
-                out=offset[j][:], in0=mean_neg[j][:], in1=rstd[j][:], op=ALU.mult
+                out=offset[q][:], in0=mean_neg[q][:], in1=rstd[q][:], op=ALU.mult
             )
 
-        def normalise(j):
-            normal[j] = work.tile([P, PAIR_T, D], F32, name="normal")
-            for t in range(PAIR_T):
-                nc.scalar.activation(
-                    out=normal[j][:, t, :],
-                    in_=y[j][:, :, t],
-                    func=ACT.Identity,
-                    bias=offset[j][:, t : t + 1],
-                    scale=rstd[j][:, t : t + 1],
-                )
+        def normalise(q):
+            normal[q] = work.tile([P, QUAD, PAIR_T, D], F32, name="normal")
+            for h in range(QUAD):
+                for t in range(PAIR_T):
+                    nc.scalar.activation(
+                        out=normal[q][:, h, t, :],
+                        in_=y[q][:, h, :, t],
+                        func=ACT.Identity,
+                        bias=offset[q][:, h, t : t + 1],
+                        scale=rstd[q][:, h, t : t + 1],
+                    )
 
-        def gain(j):
-            gained[j] = work.tile([P, PAIR_T, D], F32, name="gained")
+        def over_tokens(v):
+            return vectors_ps[:, v, :].unsqueeze(1).to_broadcast([P, QUAD * PAIR_T, D])
+
+        def gain(q):
+            gained[q] = work.tile([P, QUAD * PAIR_T, D], F32, name="gained")
             nc.vector.tensor_tensor(
-                out=gained[j][:],
-                in0=normal[j][:],
-                in1=vectors_ps[:, 0, :].unsqueeze(1).to_broadcast([P, PAIR_T, D]),
+                out=gained[q][:],
+                in0=normal[q][:].rearrange("p h t f -> p (h t) f"),
+                in1=over_tokens(0),
                 op=ALU.mult,
             )
 
-        def shift_store(j):
-            first = j - j % STORE_PAIRS
-            if j == first:
-                result[first] = results.tile([P, STORE_PAIRS * PAIR_T, D], F32, name="result")
-            nc.vector.tensor_tensor(
-                out=result[first][:, (j - first) * PAIR_T : (j - first + 1) * PAIR_T, :],
-                in0=gained[j][:],
-                in1=vectors_ps[:, 1, :].unsqueeze(1).to_broadcast([P, PAIR_T, D]),
-                op=ALU.add,
-            )
-            if j == first + STORE_PAIRS - 1:
-                nc.sync.dma_start(
-                    out=out_dram[:, first * PAIR_T : (j + 1) * PAIR_T, :], in_=result[first][:]
-                )
+        def shift_store(q):
+            result = results.tile([P, QUAD * PAIR_T, D], F32, name="result")
+            nc.vector.tensor_tensor(out=result[:], in0=gained[q][:], in1=over_tokens(1), op=ALU.add)
+            t0 = q * QUAD * PAIR_T
+            nc.sync.dma_start(out=out_dram[:, t0 : t0 + QUAD * PAIR_T, :], in_=result[:])
 
-        def run(stage, j):
+        def run(stage, q):
+            if 0 <= q < N_QUADS:
+                stage(q)
+
+        def run_pair(stage, j):
             if 0 <= j < N_PAIRS:
                 stage(j)
 
         transposes(0)
-        for turn in range(N_PAIRS + LAST_LAG + 1):
-            run(transposes, turn + 1)
-            if turn == 0:
+        for turn in range(N_PAIRS + LAST_LAG):
+            even = turn % 2 == 0
+            run_pair(transposes, turn + 1)
+            if turn == 1:
                 spread_vectors()
-            run(mx_passes, turn - 2)
-            run(rstd_of, turn - 4)
-            run(mean_neg_of, turn - 4)
-            run(copy_out, turn)
+            run_pair(mx_passes, turn - 2)
+            if even:
+                run(rstd_of, (turn - 6) // 2)
+            run_pair(copy_out, turn)
             if turn == 0:
+                lay_out_upper()
+            if turn == 1:
                 nc.scalar.copy(out=bias_bc[:], in_=vectors_ps[:, 2, :])
-            run(normalise, turn - 5)
-            run(quantise, turn - 1)
-            run(add_residual, turn - 3)
-            run(shift_store, turn - LAST_LAG)
-            run(statistics, turn - 3)
-            run(gain, turn - 6)
-            run(offset_of, turn - 4)
-            run(add_bias_to_residual, turn - 2)
+            if even:
+                run(offset_of, (turn - 6) // 2)
+                run(normalise, (turn - 6) // 2)
+            run_pair(quantise, turn - 1)
+            if turn == 1:
+                quantise_weights()
+            if even:
+                run(add_residual, (turn - 4) // 2)
+                run(shift_store, (turn - LAST_LAG) // 2)
+            run_pair(statistics, turn - 4)
+            if not even:
+                run(gain, (turn - 7) // 2)
+            if even:
+                run(add_bias_to_residual, (turn - 2) // 2)

@@ -29,8 +29,9 @@ N_PAIRS = T_ALL // PAIR_T
 BANK_HEAD_PAIRS = 2
 PAIR_BANKS = HEAD_PAIRS // BANK_HEAD_PAIRS
 FIRST_CHUNK_T = 2
+EARLY_T = 24
+EARLY_CHUNK_T = 4
 MAX_CHUNK_T = 8
-RES_CHUNK_T = 8
 QUAD = 2
 QUAD_T = QUAD * PAIR_T
 N_QUADS = N_PAIRS // QUAD
@@ -40,7 +41,7 @@ LAST_LAG = 8
 def chunk_sizes():
     sizes = [FIRST_CHUNK_T]
     while sum(sizes) < T_ALL:
-        sizes.append(min(sum(sizes), MAX_CHUNK_T))
+        sizes.append(min(sum(sizes), EARLY_CHUNK_T if sum(sizes) < EARLY_T else MAX_CHUNK_T))
     return sizes
 
 
@@ -58,7 +59,7 @@ def tile_multiheadattention_pb_t_kernel(
         quant = ctx.enter_context(tc.tile_pool(name="quant", bufs=3))
         work = ctx.enter_context(tc.tile_pool(name="work", bufs=3))
         stats = ctx.enter_context(tc.tile_pool(name="stats", bufs=3))
-        biased = ctx.enter_context(tc.tile_pool(name="biased", bufs=2))
+        biased = ctx.enter_context(tc.tile_pool(name="biased", bufs=3))
         results = ctx.enter_context(tc.tile_pool(name="results", bufs=12))
         psum_t = ctx.enter_context(tc.psum_pool(name="psum_t", bufs=5))
         psum_y = ctx.enter_context(tc.psum_pool(name="psum_y", bufs=2))
@@ -100,12 +101,13 @@ def tile_multiheadattention_pb_t_kernel(
             for s in range(chunk_t // PAIR_T):
                 x_words.append(chunk_words[:, :, s * PAIR_T * WORDS : (s + 1) * PAIR_T * WORDS])
             t0 += chunk_t
-            r0 = len(res_rows) * QUAD_T
-            if 2 * (t0 - r0) >= RES_CHUNK_T:
-                res_sb = loads.tile([P, RES_CHUNK_T, D], BF16, name="res%d" % c)
-                nc.sync.dma_start(out=res_sb[:], in_=res_dram[:, r0 : r0 + RES_CHUNK_T, :])
-                for s in range(RES_CHUNK_T // QUAD_T):
-                    res_rows.append(res_sb[:, s * QUAD_T : (s + 1) * QUAD_T, :])
+            r0 = len(res_rows) * PAIR_T
+            res_t = EARLY_CHUNK_T if r0 < MAX_CHUNK_T else MAX_CHUNK_T
+            if 2 * (t0 - r0) >= res_t:
+                res_sb = loads.tile([P, res_t, D], BF16, name="res%d" % c)
+                nc.sync.dma_start(out=res_sb[:], in_=res_dram[:, r0 : r0 + res_t, :])
+                for s in range(res_t // PAIR_T):
+                    res_rows.append(res_sb[:, s * PAIR_T : (s + 1) * PAIR_T, :])
 
         vectors_ps = psum_c.tile([P, 3, D], F32)
         bias_bc = consts.tile([P, D], BF16)
@@ -127,9 +129,10 @@ def tile_multiheadattention_pb_t_kernel(
         lower, upper = slice(0, WORDS), slice(WORDS, P)
         w_spread = w_rows[:].rearrange("p a v f -> p a f v")
         nc.vector.tensor_copy(out=w_grouped[lower, :, :, 0, :], in_=w_spread[lower])
+        nc.vector.tensor_copy(out=w_grouped[upper, 3:, :, 1, :], in_=w_spread[upper, 3:])
 
         def lay_out_upper():
-            nc.scalar.copy(out=w_grouped[upper, :, :, 1, :], in_=w_spread[upper])
+            nc.scalar.copy(out=w_grouped[upper, :3, :, 1, :], in_=w_spread[upper, :3])
 
         w_codes = consts.tile([P, HEAD_PAIRS, PAIR_T * D], U32, align_bytes=64)
         w_scales = consts.tile([P, HEAD_PAIRS, PAIR_T * D], U8, align_bytes=64)
@@ -175,38 +178,33 @@ def tile_multiheadattention_pb_t_kernel(
             )
 
         def mx_passes(j):
-            q, h = divmod(j, QUAD)
-            if h == 0:
-                y_ps[q] = psum_y.tile([P, QUAD, D, PAIR_T], F32, name="y_ps")
-            for a, start, stop in ((0, True, True),) + tuple(
-                (a, a == 0, a == HEAD_PAIRS - 1) for a in range(HEAD_PAIRS)
-            ):
+            y_ps[j] = psum_y.tile([P, D, PAIR_T], F32, name="y_ps")
+            for a in range(HEAD_PAIRS):
                 nc.tensor.matmul_mx(
-                    out=y_ps[q][:, h].rearrange("p f t -> p (f t)"),
+                    out=y_ps[j][:].rearrange("p f t -> p (f t)"),
                     lhsT=x_codes[j][:, a, :].bitcast(FP8X4),
                     lhsT_scale=x_scales[j][:, a, :],
                     rhs=w_codes[:, a, :].bitcast(FP8X4),
                     rhs_scale=w_scales[:, a, :],
-                    start=start,
-                    stop=stop,
+                    start=(a == 0),
+                    stop=(a == HEAD_PAIRS - 1),
                 )
 
-        def add_bias_to_residual(q):
-            res_bias[q] = biased.tile([P, QUAD, D, PAIR_T], F32, name="res_bias")
+        def add_bias_to_residual(j):
+            res_bias[j] = biased.tile([P, D, PAIR_T], F32, name="res_bias")
             nc.gpsimd.tensor_tensor(
-                out=res_bias[q][:],
-                in0=res_rows[q].rearrange("p (h t) f -> p h f t", h=QUAD),
-                in1=bias_bc[:].unsqueeze(1).unsqueeze(3).to_broadcast([P, QUAD, D, PAIR_T]),
+                out=res_bias[j][:],
+                in0=res_rows[j].rearrange("p t f -> p f t"),
+                in1=bias_bc[:].unsqueeze(2).to_broadcast([P, D, PAIR_T]),
                 op=ALU.add,
             )
 
-        def add_residual(q):
-            y[q] = work.tile([P, QUAD, D, PAIR_T], F32, name="y")
+        def add_residual(j):
+            q, h = divmod(j, QUAD)
+            if h == 0:
+                y[q] = work.tile([P, QUAD, D, PAIR_T], F32, name="y")
             nc.vector.tensor_tensor(
-                out=y[q][:],
-                in0=y_ps[q][:],
-                in1=res_bias[q][:],
-                op=ALU.add,
+                out=y[q][:, h], in0=y_ps[j][:], in1=res_bias[j][:], op=ALU.add
             )
 
         def statistics(j):
@@ -236,17 +234,18 @@ def tile_multiheadattention_pb_t_kernel(
                 out=offset[q][:], in0=mean_neg[q][:], in1=rstd[q][:], op=ALU.mult
             )
 
-        def normalise(q):
-            normal[q] = work.tile([P, QUAD, PAIR_T, D], F32, name="normal")
-            for h in range(QUAD):
-                for t in range(PAIR_T):
-                    nc.scalar.activation(
-                        out=normal[q][:, h, t, :],
-                        in_=y[q][:, h, :, t],
-                        func=ACT.Identity,
-                        bias=offset[q][:, h, t : t + 1],
-                        scale=rstd[q][:, h, t : t + 1],
-                    )
+        def normalise(j):
+            q, h = divmod(j, QUAD)
+            if h == 0:
+                normal[q] = work.tile([P, QUAD, PAIR_T, D], F32, name="normal")
+            for t in range(PAIR_T):
+                nc.scalar.activation(
+                    out=normal[q][:, h, t, :],
+                    in_=y[q][:, h, :, t],
+                    func=ACT.Identity,
+                    bias=offset[q][:, h, t : t + 1],
+                    scale=rstd[q][:, h, t : t + 1],
+                )
 
         def over_tokens(v):
             return vectors_ps[:, v, :].unsqueeze(1).to_broadcast([P, QUAD * PAIR_T, D])
@@ -281,24 +280,23 @@ def tile_multiheadattention_pb_t_kernel(
             if turn == 1:
                 spread_vectors()
             run_pair(mx_passes, turn - 2)
-            if even:
-                run(rstd_of, (turn - 6) // 2)
+            if not even:
+                run(rstd_of, (turn - 5) // 2)
             run_pair(copy_out, turn)
             if turn == 0:
                 lay_out_upper()
             if turn == 1:
                 nc.scalar.copy(out=bias_bc[:], in_=vectors_ps[:, 2, :])
-            if even:
-                run(offset_of, (turn - 6) // 2)
-                run(normalise, (turn - 6) // 2)
+            if not even:
+                run(offset_of, (turn - 5) // 2)
+            run_pair(normalise, turn - 5)
             run_pair(quantise, turn - 1)
             if turn == 1:
                 quantise_weights()
+            run_pair(add_residual, turn - 3)
             if even:
-                run(add_residual, (turn - 4) // 2)
                 run(shift_store, (turn - LAST_LAG) // 2)
-            run_pair(statistics, turn - 4)
-            if not even:
+            else:
                 run(gain, (turn - 7) // 2)
-            if even:
-                run(add_bias_to_residual, (turn - 2) // 2)
+            run_pair(statistics, turn - 3)
+            run_pair(add_bias_to_residual, turn - 2)

@@ -59,7 +59,7 @@ def tile_multiheadattention_pb_t_kernel(
         quant = ctx.enter_context(tc.tile_pool(name="quant", bufs=3))
         work = ctx.enter_context(tc.tile_pool(name="work", bufs=3))
         stats = ctx.enter_context(tc.tile_pool(name="stats", bufs=3))
-        biased = ctx.enter_context(tc.tile_pool(name="biased", bufs=3))
+        biased = ctx.enter_context(tc.tile_pool(name="biased", bufs=2))
         results = ctx.enter_context(tc.tile_pool(name="results", bufs=12))
         psum_t = ctx.enter_context(tc.psum_pool(name="psum_t", bufs=5))
         psum_y = ctx.enter_context(tc.psum_pool(name="psum_y", bufs=2))
@@ -287,16 +287,16 @@ def tile_multiheadattention_pb_t_kernel(
                 lay_out_upper()
             if turn == 1:
                 nc.scalar.copy(out=bias_bc[:], in_=vectors_ps[:, 2, :])
-            if not even:
-                run(offset_of, (turn - 5) // 2)
-            run_pair(normalise, turn - 5)
+            run_pair(add_residual, turn - 3)
             run_pair(quantise, turn - 1)
             if turn == 1:
                 quantise_weights()
-            run_pair(add_residual, turn - 3)
             if even:
                 run(shift_store, (turn - LAST_LAG) // 2)
             else:
                 run(gain, (turn - 7) // 2)
             run_pair(statistics, turn - 3)
-            run_pair(add_bias_to_residual, turn - 2)
+            run_pair(add_bias_to_residual, turn - 1)
+            if not even:
+                run(offset_of, (turn - 5) // 2)
+            run_pair(normalise, turn - 5)

from contextlib import ExitStack

import concourse.mybir as mybir
from concourse.masks import make_identity

FLOPS = 2 * 8192 * 1024 * 128

F32 = mybir.dt.float32
BF16 = mybir.dt.bfloat16
U32 = mybir.dt.uint32
U8 = mybir.dt.uint8
FP8X4 = mybir.dt.float8_e4m3fn_x4
ALU = mybir.AluOpType
ACT = mybir.ActivationFunctionType

P = 128
HEADS = 8
DV = 128
D = 128
TOKENS = 8192
LN_EPS = 1e-5

T_ALL = TOKENS // P
WORDS = DV // 2
HEAD_PAIRS = HEADS // 2
PACK = 4
PAIR_T = 2
N_PAIRS = T_ALL // PAIR_T
BANK_HEAD_PAIRS = 2
PAIR_BANKS = HEAD_PAIRS // BANK_HEAD_PAIRS
FIRST_CHUNK_T = 2
EARLY_T = 24
EARLY_CHUNK_T = 4
MAX_CHUNK_T = 8
QUAD = 2
QUAD_T = QUAD * PAIR_T
N_QUADS = N_PAIRS // QUAD
LAST_LAG = 8


def chunk_sizes():
    sizes = [FIRST_CHUNK_T]
    while sum(sizes) < T_ALL:
        sizes.append(min(sum(sizes), EARLY_CHUNK_T if sum(sizes) < EARLY_T else MAX_CHUNK_T))
    return sizes


def tile_multiheadattention_pb_t_kernel(
    tc, attn_out, residual, proj_w, proj_b, ln_g, ln_b, out
):
    nc = tc.nc
    x_dram = attn_out.rearrange("h (p t) j -> p h t j", t=T_ALL)
    res_dram = residual.rearrange("(p t) f -> p t f", t=T_ALL)
    out_dram = out.rearrange("(p t) f -> p t f", t=T_ALL)

    with ExitStack() as ctx:
        consts = ctx.enter_context(tc.tile_pool(name="consts", bufs=1))
        loads = ctx.enter_context(tc.tile_pool(name="loads", bufs=1))
        quant = ctx.enter_context(tc.tile_pool(name="quant", bufs=3))
        work = ctx.enter_context(tc.tile_pool(name="work", bufs=3))
        stats = ctx.enter_context(tc.tile_pool(name="stats", bufs=3))
        biased = ctx.enter_context(tc.tile_pool(name="biased", bufs=2))
        results = ctx.enter_context(tc.tile_pool(name="results", bufs=12))
        psum_t = ctx.enter_context(tc.psum_pool(name="psum_t", bufs=5))
        psum_y = ctx.enter_context(tc.psum_pool(name="psum_y", bufs=2))
        psum_c = ctx.enter_context(tc.psum_pool(name="psum_c", bufs=1))
        ctx.enter_context(tc.manual_schedule())

        vectors = consts.tile([P, 3, D], BF16)
        nc.vector.memset(vectors[:], 0.0)
        ones = consts.tile([P, P], BF16)
        nc.vector.memset(ones[:], 1.0)
        ident = consts.tile([P, P], F32)
        make_identity(nc, ident[:])

        w_rows = consts.tile([P, HEAD_PAIRS, PACK, D], BF16)

        def load_weights():
            for s in range(PAIR_T):
                nc.sync.dma_start(
                    out=w_rows[s * WORDS : (s + 1) * WORDS].rearrange(
                        "p a (i e) f -> p (a i) (e f)", i=2
                    ),
                    in_=proj_w.rearrange("(h w e) f -> w h (e f)", h=HEADS, e=2),
                )

        x_words = []
        res_rows = []
        t0 = 0
        for c, chunk_t in enumerate(chunk_sizes()):
            x_sb = loads.tile([P, HEADS * chunk_t * DV], BF16, name="x%d" % c)
            nc.sync.dma_start(
                out=x_sb[:].rearrange("p (h t j) -> p h t j", h=HEADS, t=chunk_t),
                in_=x_dram[:, :, t0 : t0 + chunk_t, :],
            )
            if c == 0:
                load_weights()
                for v, vector in enumerate((ln_g, ln_b, proj_b)):
                    nc.sync.dma_start(out=vectors[0:1, v, :], in_=vector.unsqueeze(0))
            chunk_words = x_sb[:].bitcast(F32).rearrange("p (h w) -> p h w", h=HEADS)
            for s in range(chunk_t // PAIR_T):
                x_words.append(chunk_words[:, :, s * PAIR_T * WORDS : (s + 1) * PAIR_T * WORDS])
            t0 += chunk_t
            r0 = len(res_rows) * PAIR_T
            res_t = EARLY_CHUNK_T if r0 < MAX_CHUNK_T else MAX_CHUNK_T
            if 2 * (t0 - r0) >= res_t:
                res_sb = loads.tile([P, res_t, D], BF16, name="res%d" % c)
                nc.sync.dma_start(out=res_sb[:], in_=res_dram[:, r0 : r0 + res_t, :])
                for s in range(res_t // PAIR_T):
                    res_rows.append(res_sb[:, s * PAIR_T : (s + 1) * PAIR_T, :])

        vectors_ps = psum_c.tile([P, 3, D], F32)
        bias_bc = consts.tile([P, D], BF16)

        def spread_vectors():
            nc.tensor.matmul(
                vectors_ps[:].rearrange("p v f -> p (v f)"),
                lhsT=ones[:],
                rhs=vectors[:].rearrange("p v f -> p (v f)"),
                start=True,
                stop=True,
            )

        eps = consts.tile([P, 1], F32)
        nc.vector.memset(eps[:], LN_EPS)

        w_grouped = consts.tile([P, HEAD_PAIRS, D, PAIR_T, PACK], BF16, align_bytes=64)
        nc.vector.memset(w_grouped[:], 0.0)
        lower, upper = slice(0, WORDS), slice(WORDS, P)
        w_spread = w_rows[:].rearrange("p a v f -> p a f v")
        nc.vector.tensor_copy(out=w_grouped[lower, :, :, 0, :], in_=w_spread[lower])
        nc.vector.tensor_copy(out=w_grouped[upper, 3:, :, 1, :], in_=w_spread[upper, 3:])

        def lay_out_upper():
            nc.scalar.copy(out=w_grouped[upper, :3, :, 1, :], in_=w_spread[upper, :3])

        w_codes = consts.tile([P, HEAD_PAIRS, PAIR_T * D], U32, align_bytes=64)
        w_scales = consts.tile([P, HEAD_PAIRS, PAIR_T * D], U8, align_bytes=64)

        def quantise_weights():
            nc.vector.quantize_mx(
                out=w_codes[:].rearrange("p a n -> p (a n)").bitcast(FP8X4),
                scales=w_scales[:].rearrange("p a n -> p (a n)"),
                in_=w_grouped[:].rearrange("p a f s v -> p (a f s v)"),
            )

        xt_banks, grouped, x_codes, x_scales, y_ps = {}, {}, {}, {}, {}
        res_bias, y, stat, mean_neg, rstd, offset = {}, {}, {}, {}, {}, {}
        normal, gained = {}, {}

        def transposes(j):
            for b in range(PAIR_BANKS):
                xt = psum_t.tile([P, BANK_HEAD_PAIRS, 2, P], F32, name="xt")
                for u in range(BANK_HEAD_PAIRS):
                    for i in range(2):
                        head = 2 * (b * BANK_HEAD_PAIRS + u) + i
                        nc.tensor.transpose(xt[:, u, i, :], x_words[j][:, head, :], ident[:])
                xt_banks[j, b] = xt

        def copy_out(j):
            grouped[j] = quant.tile([P, HEAD_PAIRS * P * PACK], BF16, align_bytes=64, name="grouped")
            grouped_words = grouped[j][:].bitcast(F32).rearrange(
                "p (a c i) -> p a c i", a=HEAD_PAIRS, i=2
            )
            for b in range(PAIR_BANKS):
                nc.scalar.copy(
                    out=grouped_words[:, b * BANK_HEAD_PAIRS : (b + 1) * BANK_HEAD_PAIRS, :, :],
                    in_=xt_banks[j, b][:].rearrange("p u i c -> p u c i"),
                )

        def quantise(j):
            x_codes[j] = quant.tile([P, HEAD_PAIRS, P], U32, align_bytes=64, name="x_codes")
            x_scales[j] = quant.tile([P, HEAD_PAIRS, P], U8, align_bytes=64, name="x_scales")
            nc.vector.quantize_mx(
                out=x_codes[j][:].rearrange("p a c -> p (a c)").bitcast(FP8X4),
                scales=x_scales[j][:].rearrange("p a c -> p (a c)"),
                in_=grouped[j][:],
            )

        def mx_passes(j):
            y_ps[j] = psum_y.tile([P, D, PAIR_T], F32, name="y_ps")
            for a in range(HEAD_PAIRS):
                nc.tensor.matmul_mx(
                    out=y_ps[j][:].rearrange("p f t -> p (f t)"),
                    lhsT=x_codes[j][:, a, :].bitcast(FP8X4),
                    lhsT_scale=x_scales[j][:, a, :],
                    rhs=w_codes[:, a, :].bitcast(FP8X4),
                    rhs_scale=w_scales[:, a, :],
                    start=(a == 0),
                    stop=(a == HEAD_PAIRS - 1),
                )

        def add_bias_to_residual(j):
            res_bias[j] = biased.tile([P, D, PAIR_T], F32, name="res_bias")
            nc.gpsimd.tensor_tensor(
                out=res_bias[j][:],
                in0=res_rows[j].rearrange("p t f -> p f t"),
                in1=bias_bc[:].unsqueeze(2).to_broadcast([P, D, PAIR_T]),
                op=ALU.add,
            )

        def add_residual(j):
            q, h = divmod(j, QUAD)
            if h == 0:
                y[q] = work.tile([P, QUAD, D, PAIR_T], F32, name="y")
            nc.vector.tensor_tensor(
                out=y[q][:, h], in0=y_ps[j][:], in1=res_bias[j][:], op=ALU.add
            )

        def statistics(j):
            q, h = divmod(j, QUAD)
            if h == 0:
                stat[q] = stats.tile([P, QUAD, PAIR_T, 3], F32, name="stat")
            nc.vector.bn_stats(
                out=stat[q][:, h].rearrange("p t v -> p (t v)"),
                in_=y[q][:, h].rearrange("p f t -> p (f t)"),
            )

        def rstd_of(q):
            rstd[q] = stats.tile([P, QUAD, PAIR_T], F32, name="rstd")
            nc.scalar.activation(
                out=rstd[q][:],
                in_=stat[q][:, :, :, 2],
                func=ACT.Abs_reciprocal_sqrt,
                bias=eps[:],
                scale=1.0 / D,
            )
            mean_neg[q] = stats.tile([P, QUAD, PAIR_T], F32, name="mean_neg")
            nc.scalar.mul(out=mean_neg[q][:], in_=stat[q][:, :, :, 1], mul=-1.0)

        def offset_of(q):
            offset[q] = stats.tile([P, QUAD, PAIR_T], F32, name="offset")
            nc.gpsimd.tensor_tensor(
                out=offset[q][:], in0=mean_neg[q][:], in1=rstd[q][:], op=ALU.mult
            )

        def normalise(j):
            q, h = divmod(j, QUAD)
            if h == 0:
                normal[q] = work.tile([P, QUAD, PAIR_T, D], F32, name="normal")
            for t in range(PAIR_T):
                nc.scalar.activation(
                    out=normal[q][:, h, t, :],
                    in_=y[q][:, h, :, t],
                    func=ACT.Identity,
                    bias=offset[q][:, h, t : t + 1],
                    scale=rstd[q][:, h, t : t + 1],
                )

        def over_tokens(v):
            return vectors_ps[:, v, :].unsqueeze(1).to_broadcast([P, QUAD * PAIR_T, D])

        def gain(q):
            gained[q] = work.tile([P, QUAD * PAIR_T, D], F32, name="gained")
            nc.vector.tensor_tensor(
                out=gained[q][:],
                in0=normal[q][:].rearrange("p h t f -> p (h t) f"),
                in1=over_tokens(0),
                op=ALU.mult,
            )

        def shift_store(q):
            result = results.tile([P, QUAD * PAIR_T, D], F32, name="result")
            nc.vector.tensor_tensor(out=result[:], in0=gained[q][:], in1=over_tokens(1), op=ALU.add)
            t0 = q * QUAD * PAIR_T
            nc.sync.dma_start(out=out_dram[:, t0 : t0 + QUAD * PAIR_T, :], in_=result[:])

        def run(stage, q):
            if 0 <= q < N_QUADS:
                stage(q)

        def run_pair(stage, j):
            if 0 <= j < N_PAIRS:
                stage(j)

        transposes(0)
        for turn in range(N_PAIRS + LAST_LAG):
            even = turn % 2 == 0
            run_pair(transposes, turn + 1)
            if turn == 1:
                spread_vectors()
            run_pair(mx_passes, turn - 2)
            if not even:
                run(rstd_of, (turn - 5) // 2)
            run_pair(copy_out, turn)
            if turn == 0:
                lay_out_upper()
            if turn == 1:
                nc.scalar.copy(out=bias_bc[:], in_=vectors_ps[:, 2, :])
            run_pair(add_residual, turn - 3)
            run_pair(quantise, turn - 1)
            if turn == 1:
                quantise_weights()
            if even:
                run(shift_store, (turn - LAST_LAG) // 2)
            else:
                run(gain, (turn - 7) // 2)
            run_pair(statistics, turn - 3)
            run_pair(add_bias_to_residual, turn - 1)
            if not even:
                run(offset_of, (turn - 5) // 2)
            run_pair(normalise, turn - 5)
